import numpy as np
import ml_dtypes


def mxq(x, axis, fmt="e4m3"):
    dtype, down = {"e4m3": (ml_dtypes.float8_e4m3fn, 7), "e5m2": (ml_dtypes.float8_e5m2, 14)}[fmt]
    v = np.moveaxis(np.asarray(x, np.float32).astype(ml_dtypes.bfloat16).astype(np.float64), axis, -1)
    blocks = v.reshape(v.shape[:-1] + (-1, 32))
    amax = np.abs(blocks).max(-1, keepdims=True)
    byte = np.maximum(np.where(amax > 0, np.frexp(amax)[1] - 1 + 127, 0) - down, 1)
    scale = np.exp2(byte - 127.0)
    codes = (blocks / scale).astype(np.float32).astype(dtype).astype(np.float64)
    return np.moveaxis((codes * scale).reshape(v.shape), -1, axis)


WIDE = False


def mx_kscale(k):
    if not WIDE:
        return np.ones(k)
    levels = np.array([10, -10, 5, -5, 0])
    a = np.random.permutation(np.resize(levels, k // 512 * 4)).reshape(k // 512, 4)
    idx = np.arange(k)
    return np.exp2(a[idx // 512, idx % 128 // 32])


BF16 = ml_dtypes.bfloat16


def bf(x):
    return np.asarray(x, np.float32).astype(BF16)


def f64(x):
    return np.asarray(x).astype(np.float64)


E2M1 = np.array([0.0, 0.5, 1.0, 1.5, 2.0, 3.0, 4.0, 6.0, -0.0, -0.5, -1.0, -1.5, -2.0, -3.0, -4.0, -6.0])


def pack_weight(w, fmt):
    k, n = w.shape
    w = f64(bf(w)).reshape(k // 32, 32, n)
    amax = np.abs(w).max(1)
    if fmt == "e4m3":
        byte = np.frexp(amax)[1] - 1 + 127 - 7
    else:
        mant, ex = np.frexp(amax / 6.0)
        byte = np.where(mant > 0.5, ex, ex - 1) + 127
    byte = np.clip(np.where(amax > 0, byte, 1), 1, 254)
    scaled = (w * np.exp2(127.0 - byte)[:, None, :]).reshape(k, n).astype(np.float32)
    by_word = np.ascontiguousarray(scaled.reshape(k // 512, 128, 4, n).transpose(0, 1, 3, 2))
    if fmt == "e4m3":
        words = by_word.astype(ml_dtypes.float8_e4m3fn).view(np.uint8)
    else:
        c = by_word.astype(ml_dtypes.float4_e2m1fn).view(np.uint8) & 0xF
        words = c[..., 0::2] | (c[..., 1::2] << 4)
    return np.ascontiguousarray(words), np.ascontiguousarray(byte.astype(np.uint8).reshape(k // 512, 16, n))


def unpack_weight(words, scales, fmt):
    g, p, n, _ = words.shape
    if fmt == "e4m3":
        vals = np.ascontiguousarray(words).view(ml_dtypes.float8_e4m3fn).astype(np.float64)
    else:
        nib = np.empty((g, p, n, 4), np.uint8)
        nib[..., 0::2] = words & 0xF
        nib[..., 1::2] = words >> 4
        vals = E2M1[nib]
    vals = vals * np.repeat(np.exp2(scales.astype(np.float64) - 127.0), 8, axis=1)[..., None]
    return vals.transpose(0, 1, 3, 2).reshape(g * 512, n)


N, D, C, M = 128, 2048, 64, 64


def setup_inputs():
    s = mx_kscale(D)
    x = bf(np.random.standard_normal((N, D)) * s)
    x_var = bf(0.1 + 4.0 * np.random.standard_normal((N, D)) ** 2)
    stack = (np.random.standard_normal((C, M, D)) * 0.5 / np.sqrt(D) / s).swapaxes(1, 2)
    words, scales = pack_weight(stack.reshape(-1, M), "e4m3")
    proto_var = bf(0.1 + 4.0 * np.random.standard_normal((C, M, D)) ** 2)
    return {"x": x,
            "x_var": x_var,
            "prototypes_words": words,
            "prototypes_scales": scales,
            "proto_var": proto_var}


def reference(x, x_var, prototypes_words, prototypes_scales, proto_var):
    x, x_var, proto_var = f64(x), f64(x_var), f64(proto_var)
    lamda = 1.0 / x.shape[-1]
    dot = (mxq(x, 1, "e4m3") @ unpack_weight(prototypes_words, prototypes_scales, "e4m3").reshape(C, D, M).swapaxes(1, 2).reshape(C * M, D).T).reshape(N, C, M)
    cross = (mxq(np.sqrt(x_var), 1, "e4m3") @ mxq(np.sqrt(proto_var).reshape(C * M, D), 1, "e4m3").T).reshape(N, C, M)
    w2 = (2.0 - 2.0 * dot
          + lamda * (np.sum(x_var, axis=-1)[:, None, None]
                     + np.sum(proto_var, axis=-1)[None, :, :]
                     - 2.0 * cross))
    return -w2

@@ -1,0 +1,322 @@
+from contextlib import ExitStack
+
+import concourse.mybir as mybir
+from concourse.masks import make_identity
+
+F32 = mybir.dt.float32
+BF16 = mybir.dt.bfloat16
+U32 = mybir.dt.uint32
+U8 = mybir.dt.uint8
+I32 = mybir.dt.int32
+FP8X4 = mybir.dt.float8_e4m3fn_x4
+ALU = mybir.AluOpType
+SQRT = mybir.ActivationFunctionType.Sqrt
+
+P = 128
+D = 2048
+PACK = 4
+K_PASS = P * PACK
+PASSES = D // K_PASS
+CLASSES = 64
+PER_CLASS = 64
+GROUP = 512
+N_GROUPS = CLASSES * PER_CLASS // GROUP
+GROUP_CLASSES = GROUP // PER_CLASS
+PAIR = 2 * P
+PAIRS = GROUP // PAIR
+LAM = 1.0 / D
+ROW_GROUPS = 3
+WORD_GROUPS = 4
+
+FLOPS = 2 * 2 * P * CLASSES * PER_CLASS * D
+
+
+def tile_probprotoseghead_w_e_kernel(
+    tc, x, x_var, prototypes_words, prototypes_scales, proto_var, out
+):
+    nc = tc.nc
+    var_rows = proto_var.rearrange("c m d -> (c m) d")
+    word_view = prototypes_words.rearrange("(c g) p m t -> g p c (m t)", g=PASSES)
+    scale_view = prototypes_scales.rearrange("(c g) q m -> q g c m", g=PASSES)
+    out_cols = out.rearrange("n c m -> n (c m)")
+
+    with ExitStack() as stack:
+        const = stack.enter_context(tc.tile_pool(name="const", bufs=1))
+        rows_pool = stack.enter_context(tc.tile_pool(name="rows", bufs=ROW_GROUPS * PAIRS))
+        words_pool = stack.enter_context(tc.tile_pool(name="words", bufs=WORD_GROUPS))
+        grouped_pool = stack.enter_context(tc.tile_pool(name="grouped", bufs=2))
+        codes_pool = stack.enter_context(tc.tile_pool(name="codes", bufs=3))
+        work = stack.enter_context(tc.tile_pool(name="work", bufs=2))
+        banks = stack.enter_context(tc.psum_pool(name="banks", bufs=4))
+        acc_pool = stack.enter_context(tc.psum_pool(name="acc", bufs=2))
+        spread_pool = stack.enter_context(tc.psum_pool(name="spread", bufs=2))
+        stack.enter_context(tc.manual_schedule())
+
+        def live(group):
+            return 0 <= group < N_GROUPS
+
+        def transpose_four(bank, blocks):
+            for slot, block in enumerate(blocks):
+                nc.tensor.transpose(bank[:, slot * P : (slot + 1) * P], block, ident[:])
+
+        def root(bank, dest, scale):
+            nc.scalar.activation(
+                out=dest.rearrange("p c (u e) -> p c u e", u=2),
+                in_=bank[:].bitcast(BF16).rearrange("p (u c e) -> p c u e", u=2, e=2),
+                func=SQRT,
+                scale=scale,
+            )
+
+        def sum_row(row, total):
+            junk = work.tile([P, D // 2], F32, name="junk")
+            nc.vector.scalar_tensor_tensor(
+                out=junk[:],
+                in0=row[:, : D // 2],
+                scalar=1.0,
+                in1=row[:, D // 2 :],
+                op0=ALU.mult,
+                op1=ALU.add,
+                accum_out=total,
+            )
+
+        def quantise(grouped, codes, planes):
+            nc.vector.quantize_mx(out=codes.bitcast(FP8X4), scales=planes, in_=grouped)
+
+        rows_of = {}
+        words_of = {}
+
+        def load_rows(group):
+            for pair in range(PAIRS):
+                rows = rows_pool.tile([P, 2, D], BF16, name="rows")
+                first = group * GROUP + pair * PAIR
+                nc.sync.dma_start(
+                    out=rows[:],
+                    in_=var_rows[first : first + PAIR, :].rearrange("(t p) d -> p t d", p=P),
+                )
+                rows_of[(group, pair)] = rows
+
+        def load_words(group):
+            words = words_pool.tile([P, PASSES, GROUP], U32, name="words", align_bytes=64)
+            first = group * GROUP_CLASSES
+            for g in range(PASSES):
+                nc.sync.dma_start(
+                    out=words[:, g, :].bitcast(I32).rearrange("p (c w) -> p c w", c=GROUP_CLASSES),
+                    in_=word_view[g][:, first : first + GROUP_CLASSES, :].bitcast(I32),
+                )
+            words_of[group] = words
+
+        proto_planes = const.tile([P, CLASSES * PER_CLASS], U8, name="proto_planes", align_bytes=64)
+        nc.vector.memset(proto_planes[:].bitcast(I32), 0)
+        ident = const.tile([P, P], F32, name="ident")
+        make_identity(nc, ident[:])
+        for quadrant in range(4):
+            for r in range(4):
+                first = 32 * quadrant + r
+                nc.gpsimd.dma_start(
+                    out=proto_planes[first : 32 * quadrant + 16 : 4, :]
+                    .bitcast(F32)
+                    .rearrange("g (c w) -> g c w", c=CLASSES),
+                    in_=scale_view[4 * quadrant + r].bitcast(F32),
+                )
+
+        xv_rows = const.tile([P, D], BF16, name="xv_rows")
+        nc.sync.dma_start(out=xv_rows[:], in_=x_var)
+        x_rows = const.tile([P, D], BF16, name="x_rows")
+        nc.sync.dma_start(out=x_rows[:], in_=x)
+        load_rows(0)
+        for group in range(1, ROW_GROUPS):
+            load_rows(group)
+            load_words(group - 1)
+
+        xv_grouped = const.tile([P, PASSES, P, PACK], BF16, name="xv_grouped", align_bytes=64)
+        x_grouped = const.tile([P, PASSES, P, PACK], BF16, name="x_grouped", align_bytes=64)
+        xv_codes = const.tile([P, PASSES, P], U32, name="xv_codes", align_bytes=64)
+        x_codes = const.tile([P, PASSES, P], U32, name="x_codes", align_bytes=64)
+        xv_planes = const.tile([P, PASSES, P], U8, name="xv_planes", align_bytes=64)
+        x_planes = const.tile([P, PASSES, P], U8, name="x_planes", align_bytes=64)
+        xv_sum = const.tile([P, 1], F32, name="xv_sum")
+        pixel_term = const.tile([P, 1], F32, name="pixel_term")
+
+        xv_words = xv_rows[:].bitcast(F32)
+        x_words = x_rows[:].bitcast(F32)
+        for half in range(2):
+            bank = banks.tile([P, GROUP], F32, name="bank")
+            transpose_four(
+                bank,
+                [
+                    xv_words[:, (2 * g + u) * P : (2 * g + u + 1) * P]
+                    for u in range(2)
+                    for g in (2 * half, 2 * half + 1)
+                ],
+            )
+            root(
+                bank,
+                xv_grouped[:, 2 * half : 2 * half + 2, :, :].rearrange("p g n t -> p (g n) t"),
+                LAM * LAM,
+            )
+        sum_row(xv_rows, xv_sum[:])
+        nc.vector.tensor_scalar(
+            out=pixel_term[:], in0=xv_sum[:], scalar1=LAM, scalar2=2.0, op0=ALU.mult, op1=ALU.add
+        )
+        for half in range(2):
+            bank = banks.tile([P, GROUP], F32, name="bank")
+            transpose_four(
+                bank,
+                [
+                    x_words[:, 2 * P * g + u : 2 * P * (g + 1) : 2]
+                    for u in range(2)
+                    for g in (2 * half, 2 * half + 1)
+                ],
+            )
+            nc.vector.tensor_copy(
+                out=x_grouped[:, 2 * half : 2 * half + 2, :, :]
+                .bitcast(F32)
+                .rearrange("p g n u -> p (g n) u"),
+                in_=bank[:].rearrange("p (u c) -> p c u", u=2),
+            )
+        quantise(
+            xv_grouped[:].rearrange("p g n t -> p (g n t)"),
+            xv_codes[:].rearrange("p g n -> p (g n)"),
+            xv_planes[:].rearrange("p g n -> p (g n)"),
+        )
+        quantise(
+            x_grouped[:].rearrange("p g n t -> p (g n t)"),
+            x_codes[:].rearrange("p g n -> p (g n)"),
+            x_planes[:].rearrange("p g n -> p (g n)"),
+        )
+
+        grouped_of = {}
+        sums_of = {}
+        codes_of = {}
+        planes_of = {}
+        spread_of = {}
+        shift_of = {}
+        acc_of = {}
+
+        def transpose_and_root(group, pair):
+            rows = rows_of[(group, pair)]
+            for g in range(PASSES):
+                bank = banks.tile([P, GROUP], F32, name="bank")
+                transpose_four(
+                    bank,
+                    [
+                        rows[:, t, :].bitcast(F32)[:, (2 * g + u) * P : (2 * g + u + 1) * P]
+                        for u in range(2)
+                        for t in range(2)
+                    ],
+                )
+                root(bank, grouped_of[group][:, g, pair * PAIR : (pair + 1) * PAIR, :], 1.0)
+
+        def sum_rows(group, tile_index):
+            rows = rows_of[(group, tile_index // 2)]
+            sum_row(rows[:, tile_index % 2, :], sums_of[group][:, tile_index : tile_index + 1])
+
+        def quantise_half(group, half):
+            passes = slice(2 * half, 2 * half + 2)
+            quantise(
+                grouped_of[group][:, passes, :, :].rearrange("p g c t -> p (g c t)"),
+                codes_of[group][:, passes, :].rearrange("p g c -> p (g c)"),
+                planes_of[group][:, passes, :].rearrange("p g c -> p (g c)"),
+            )
+
+        def spread_sums(group):
+            spread = spread_pool.tile([P, GROUP], F32, name="spread")
+            for t in range(GROUP // P):
+                nc.tensor.transpose(
+                    spread[:, t * P : (t + 1) * P],
+                    sums_of[group][:, t : t + 1].to_broadcast([P, P]),
+                    ident[:],
+                )
+            spread_of[group] = spread
+
+        def make_shift(group):
+            shift = work.tile([P, GROUP], F32, name="shift")
+            nc.vector.tensor_scalar(
+                out=shift[:],
+                in0=spread_of[group][:],
+                scalar1=LAM,
+                scalar2=pixel_term[:, 0:1],
+                op0=ALU.mult,
+                op1=ALU.add,
+            )
+            shift_of[group] = shift
+
+        def multiply(group):
+            acc = acc_pool.tile([P, GROUP], F32, name="acc")
+            cols = slice(group * GROUP, (group + 1) * GROUP)
+            for g in range(PASSES):
+                nc.tensor.matmul_mx(
+                    out=acc[:],
+                    lhsT=xv_codes[:, g, :].bitcast(FP8X4),
+                    lhsT_scale=xv_planes[:, g, :],
+                    rhs=codes_of[group][:, g, :].bitcast(FP8X4),
+                    rhs_scale=planes_of[group][:, g, :],
+                    start=(g == 0),
+                    stop=False,
+                )
+            for g in range(PASSES):
+                nc.tensor.matmul_mx(
+                    out=acc[:],
+                    lhsT=x_codes[:, g, :].bitcast(FP8X4),
+                    lhsT_scale=x_planes[:, g, :],
+                    rhs=words_of[group][:, g, :].bitcast(FP8X4),
+                    rhs_scale=proto_planes[4 * g : P, cols],
+                    start=False,
+                    stop=(g == PASSES - 1),
+                )
+            acc_of[group] = acc
+
+        def finish(group):
+            result = work.tile([P, GROUP], F32, name="result")
+            nc.vector.scalar_tensor_tensor(
+                out=result[:],
+                in0=acc_of[group][:],
+                scalar=2.0,
+                in1=shift_of[group][:],
+                op0=ALU.mult,
+                op1=ALU.subtract,
+            )
+            nc.sync.dma_start(out=out_cols[:, group * GROUP : (group + 1) * GROUP], in_=result[:])
+
+        for step in range(N_GROUPS + 2):
+            rooted, quantised, multiplied = step, step - 1, step - 2
+            if live(rooted):
+                grouped_of[rooted] = grouped_pool.tile(
+                    [P, PASSES, GROUP, PACK], BF16, name="grouped", align_bytes=64
+                )
+                sums_of[rooted] = work.tile([P, GROUP // P], F32, name="sums")
+            if live(quantised):
+                codes_of[quantised] = codes_pool.tile(
+                    [P, PASSES, GROUP], U32, name="codes", align_bytes=64
+                )
+                planes_of[quantised] = codes_pool.tile(
+                    [P, PASSES, GROUP], U8, name="planes", align_bytes=64
+                )
+            if live(rooted):
+                transpose_and_root(rooted, 0)
+            if live(quantised):
+                spread_sums(quantised)
+            if live(rooted):
+                transpose_and_root(rooted, 1)
+            if live(multiplied):
+                multiply(multiplied)
+            if live(rooted):
+                sum_rows(rooted, 0)
+            if live(quantised):
+                quantise_half(quantised, 0)
+            if live(rooted):
+                sum_rows(rooted, 1)
+            if live(quantised):
+                quantise_half(quantised, 1)
+            if live(rooted):
+                sum_rows(rooted, 2)
+            if live(quantised):
+                make_shift(quantised)
+            if live(rooted):
+                sum_rows(rooted, 3)
+            if live(multiplied):
+                finish(multiplied)
+            if live(step + ROW_GROUPS):
+                load_rows(step + ROW_GROUPS)
+            if live(step + ROW_GROUPS - 1):
+                load_words(step + ROW_GROUPS - 1)

@@ -109,22 +109,24 @@ def tile_probprotoseghead_w_e_kernel(
         nc.vector.memset(proto_planes[:].bitcast(I32), 0)
         ident = const.tile([P, P], F32, name="ident")
         make_identity(nc, ident[:])
-        for quadrant in range(4):
-            for r in range(4):
-                first = 32 * quadrant + r
-                nc.gpsimd.dma_start(
-                    out=proto_planes[first : 32 * quadrant + 16 : 4, :]
-                    .bitcast(F32)
-                    .rearrange("g (c w) -> g c w", c=CLASSES),
-                    in_=scale_view[4 * quadrant + r].bitcast(F32),
-                )
 
         xv_rows = const.tile([P, D], BF16, name="xv_rows")
         nc.sync.dma_start(out=xv_rows[:], in_=x_var)
         x_rows = const.tile([P, D], BF16, name="x_rows")
         nc.sync.dma_start(out=x_rows[:], in_=x)
         load_rows(0)
-        for group in range(1, ROW_GROUPS):
+        load_rows(1)
+        for quadrant in range(4):
+            for r in range(4):
+                first = 32 * quadrant + r
+                nc.sync.dma_start(
+                    out=proto_planes[first : 32 * quadrant + 16 : 4, :]
+                    .bitcast(I32)
+                    .rearrange("g (c w) -> g c w", c=CLASSES),
+                    in_=scale_view[4 * quadrant + r].bitcast(I32),
+                )
+        load_words(0)
+        for group in range(2, ROW_GROUPS):
             load_rows(group)
             load_words(group - 1)
 

@@ -17,6 +17,7 @@ D = 2048
 PACK = 4
 K_PASS = P * PACK
 PASSES = D // K_PASS
+BLOCKS = D // 32
 CLASSES = 64
 PER_CLASS = 64
 GROUP = 512
@@ -37,7 +38,7 @@ def tile_probprotoseghead_w_e_kernel(
     nc = tc.nc
     var_rows = proto_var.rearrange("c m d -> (c m) d")
     word_view = prototypes_words.rearrange("(c g) p m t -> g p c (m t)", g=PASSES)
-    scale_view = prototypes_scales.rearrange("(c g) q m -> q g c m", g=PASSES)
+    scale_view = prototypes_scales.rearrange("(c g) q m -> (g q) c m", g=PASSES)
     out_cols = out.rearrange("n c m -> n (c m)")
 
     with ExitStack() as stack:
@@ -115,15 +116,17 @@ def tile_probprotoseghead_w_e_kernel(
         x_rows = const.tile([P, D], BF16, name="x_rows")
         nc.sync.dma_start(out=x_rows[:], in_=x)
         load_rows(0)
+        staged_scales = const.tile([BLOCKS, CLASSES * PER_CLASS], U8, name="staged_scales", align_bytes=64)
+        nc.sync.dma_start(
+            out=staged_scales[:].bitcast(I32).rearrange("b (c w) -> b c w", c=CLASSES),
+            in_=scale_view.bitcast(I32),
+        )
         load_rows(1)
-        for quadrant in range(4):
+        for g in range(PASSES):
             for r in range(4):
-                first = 32 * quadrant + r
                 nc.sync.dma_start(
-                    out=proto_planes[first : 32 * quadrant + 16 : 4, :]
-                    .bitcast(I32)
-                    .rearrange("g (c w) -> g c w", c=CLASSES),
-                    in_=scale_view[4 * quadrant + r].bitcast(I32),
+                    out=proto_planes[4 * g + r : P : 32, :].bitcast(I32),
+                    in_=staged_scales[16 * g + r : 16 * g + 16 : 4, :].bitcast(I32),
                 )
         load_words(0)
         for group in range(2, ROW_GROUPS):

@@ -26,8 +26,10 @@ GROUP_CLASSES = GROUP // PER_CLASS
 PAIR = 2 * P
 PAIRS = GROUP // PAIR
 LAM = 1.0 / D
-ROW_GROUPS = 3
-WORD_GROUPS = 4
+ROW_GROUPS = 4
+WORD_GROUPS = 6
+
+MULTIPLIED_IN_STEP = ((), (), (), (0,), (1,), (2, 3), (4,), (5, 6), (7,))
 
 FLOPS = 2 * 2 * P * CLASSES * PER_CLASS * D
 
@@ -48,9 +50,9 @@ def tile_probprotoseghead_w_e_kernel(
         grouped_pool = stack.enter_context(tc.tile_pool(name="grouped", bufs=2))
         codes_pool = stack.enter_context(tc.tile_pool(name="codes", bufs=3))
         work = stack.enter_context(tc.tile_pool(name="work", bufs=2))
-        banks = stack.enter_context(tc.psum_pool(name="banks", bufs=4))
+        banks = stack.enter_context(tc.psum_pool(name="banks", bufs=5))
         acc_pool = stack.enter_context(tc.psum_pool(name="acc", bufs=2))
-        spread_pool = stack.enter_context(tc.psum_pool(name="spread", bufs=2))
+        spread_pool = stack.enter_context(tc.psum_pool(name="spread", bufs=1))
         stack.enter_context(tc.manual_schedule())
 
         def live(group):
@@ -86,15 +88,18 @@ def tile_probprotoseghead_w_e_kernel(
         rows_of = {}
         words_of = {}
 
+        def load_pair(group, pair, pieces=1):
+            rows = rows_pool.tile([P, 2, D], BF16, name="rows")
+            first = group * GROUP + pair * PAIR
+            source = var_rows[first : first + PAIR, :].rearrange("(t p) d -> p t d", p=P)
+            for piece in range(pieces):
+                cols = slice(piece * D // pieces, (piece + 1) * D // pieces)
+                nc.sync.dma_start(out=rows[:, :, cols], in_=source[:, :, cols])
+            rows_of[(group, pair)] = rows
+
         def load_rows(group):
             for pair in range(PAIRS):
-                rows = rows_pool.tile([P, 2, D], BF16, name="rows")
-                first = group * GROUP + pair * PAIR
-                nc.sync.dma_start(
-                    out=rows[:],
-                    in_=var_rows[first : first + PAIR, :].rearrange("(t p) d -> p t d", p=P),
-                )
-                rows_of[(group, pair)] = rows
+                load_pair(group, pair)
 
         def load_words(group):
             words = words_pool.tile([P, PASSES, GROUP], U32, name="words", align_bytes=64)
@@ -111,17 +116,22 @@ def tile_probprotoseghead_w_e_kernel(
         ident = const.tile([P, P], F32, name="ident")
         make_identity(nc, ident[:])
 
+        load_pair(0, 0, pieces=PASSES)
+        load_pair(0, 1)
         xv_rows = const.tile([P, D], BF16, name="xv_rows")
         nc.sync.dma_start(out=xv_rows[:], in_=x_var)
-        x_rows = const.tile([P, D], BF16, name="x_rows")
-        nc.sync.dma_start(out=x_rows[:], in_=x)
-        load_rows(0)
-        staged_scales = const.tile([BLOCKS, CLASSES * PER_CLASS], U8, name="staged_scales", align_bytes=64)
+        load_pair(1, 0)
+        staged_scales = const.tile(
+            [BLOCKS, CLASSES * PER_CLASS], U8, name="staged_scales", align_bytes=64
+        )
         nc.sync.dma_start(
             out=staged_scales[:].bitcast(I32).rearrange("b (c w) -> b c w", c=CLASSES),
             in_=scale_view.bitcast(I32),
         )
-        load_rows(1)
+        load_pair(1, 1)
+        x_rows = const.tile([P, D], BF16, name="x_rows")
+        nc.sync.dma_start(out=x_rows[:], in_=x)
+        load_rows(2)
         for g in range(PASSES):
             for r in range(4):
                 nc.sync.dma_start(
@@ -129,9 +139,8 @@ def tile_probprotoseghead_w_e_kernel(
                     in_=staged_scales[16 * g + r : 16 * g + 16 : 4, :].bitcast(I32),
                 )
         load_words(0)
-        for group in range(2, ROW_GROUPS):
-            load_rows(group)
-            load_words(group - 1)
+        load_rows(3)
+        load_words(1)
 
         xv_grouped = const.tile([P, PASSES, P, PACK], BF16, name="xv_grouped", align_bytes=64)
         x_grouped = const.tile([P, PASSES, P, PACK], BF16, name="x_grouped", align_bytes=64)
@@ -142,53 +151,69 @@ def tile_probprotoseghead_w_e_kernel(
         xv_sum = const.tile([P, 1], F32, name="xv_sum")
         pixel_term = const.tile([P, 1], F32, name="pixel_term")
 
-        xv_words = xv_rows[:].bitcast(F32)
-        x_words = x_rows[:].bitcast(F32)
-        for half in range(2):
-            bank = banks.tile([P, GROUP], F32, name="bank")
-            transpose_four(
-                bank,
-                [
-                    xv_words[:, (2 * g + u) * P : (2 * g + u + 1) * P]
-                    for u in range(2)
-                    for g in (2 * half, 2 * half + 1)
-                ],
+        def transpose_xv_and_root():
+            xv_words = xv_rows[:].bitcast(F32)
+            for half in range(2):
+                bank = banks.tile([P, GROUP], F32, name="bank")
+                transpose_four(
+                    bank,
+                    [
+                        xv_words[:, (2 * g + u) * P : (2 * g + u + 1) * P]
+                        for u in range(2)
+                        for g in (2 * half, 2 * half + 1)
+                    ],
+                )
+                root(
+                    bank,
+                    xv_grouped[:, 2 * half : 2 * half + 2, :, :].rearrange("p g n t -> p (g n) t"),
+                    LAM * LAM,
+                )
+
+        def transpose_x_and_copy():
+            x_words = x_rows[:].bitcast(F32)
+            for half in range(2):
+                bank = banks.tile([P, GROUP], F32, name="bank")
+                transpose_four(
+                    bank,
+                    [
+                        x_words[:, 2 * P * g + u : 2 * P * (g + 1) : 2]
+                        for u in range(2)
+                        for g in (2 * half, 2 * half + 1)
+                    ],
+                )
+                nc.vector.tensor_copy(
+                    out=x_grouped[:, 2 * half : 2 * half + 2, :, :]
+                    .bitcast(F32)
+                    .rearrange("p g n u -> p (g n) u"),
+                    in_=bank[:].rearrange("p (u c) -> p c u", u=2),
+                )
+
+        def sum_xv():
+            sum_row(xv_rows, xv_sum[:])
+
+        def make_pixel_term():
+            nc.vector.tensor_scalar(
+                out=pixel_term[:],
+                in0=xv_sum[:],
+                scalar1=LAM,
+                scalar2=2.0,
+                op0=ALU.mult,
+                op1=ALU.add,
             )
-            root(
-                bank,
-                xv_grouped[:, 2 * half : 2 * half + 2, :, :].rearrange("p g n t -> p (g n) t"),
-                LAM * LAM,
+
+        def quantise_xv():
+            quantise(
+                xv_grouped[:].rearrange("p g n t -> p (g n t)"),
+                xv_codes[:].rearrange("p g n -> p (g n)"),
+                xv_planes[:].rearrange("p g n -> p (g n)"),
             )
-        sum_row(xv_rows, xv_sum[:])
-        nc.vector.tensor_scalar(
-            out=pixel_term[:], in0=xv_sum[:], scalar1=LAM, scalar2=2.0, op0=ALU.mult, op1=ALU.add
-        )
-        for half in range(2):
-            bank = banks.tile([P, GROUP], F32, name="bank")
-            transpose_four(
-                bank,
-                [
-                    x_words[:, 2 * P * g + u : 2 * P * (g + 1) : 2]
-                    for u in range(2)
-                    for g in (2 * half, 2 * half + 1)
-                ],
+
+        def quantise_x():
+            quantise(
+                x_grouped[:].rearrange("p g n t -> p (g n t)"),
+                x_codes[:].rearrange("p g n -> p (g n)"),
+                x_planes[:].rearrange("p g n -> p (g n)"),
             )
-            nc.vector.tensor_copy(
-                out=x_grouped[:, 2 * half : 2 * half + 2, :, :]
-                .bitcast(F32)
-                .rearrange("p g n u -> p (g n) u"),
-                in_=bank[:].rearrange("p (u c) -> p c u", u=2),
-            )
-        quantise(
-            xv_grouped[:].rearrange("p g n t -> p (g n t)"),
-            xv_codes[:].rearrange("p g n -> p (g n)"),
-            xv_planes[:].rearrange("p g n -> p (g n)"),
-        )
-        quantise(
-            x_grouped[:].rearrange("p g n t -> p (g n t)"),
-            x_codes[:].rearrange("p g n -> p (g n)"),
-            x_planes[:].rearrange("p g n -> p (g n)"),
-        )
 
         grouped_of = {}
         sums_of = {}
@@ -235,7 +260,7 @@ def tile_probprotoseghead_w_e_kernel(
             spread_of[group] = spread
 
         def make_shift(group):
-            shift = work.tile([P, GROUP], F32, name="shift")
+            shift = work.tile([P, GROUP], F32, name="shift", bufs=4)
             nc.vector.tensor_scalar(
                 out=shift[:],
                 in0=spread_of[group][:],
@@ -283,8 +308,9 @@ def tile_probprotoseghead_w_e_kernel(
             )
             nc.sync.dma_start(out=out_cols[:, group * GROUP : (group + 1) * GROUP], in_=result[:])
 
-        for step in range(N_GROUPS + 2):
-            rooted, quantised, multiplied = step, step - 1, step - 2
+        for step in range(N_GROUPS + 1):
+            rooted, quantised = step, step - 1
+            due = MULTIPLIED_IN_STEP[step]
             if live(rooted):
                 grouped_of[rooted] = grouped_pool.tile(
                     [P, PASSES, GROUP, PACK], BF16, name="grouped", align_bytes=64
@@ -298,14 +324,6 @@ def tile_probprotoseghead_w_e_kernel(
                     [P, PASSES, GROUP], U8, name="planes", align_bytes=64
                 )
             if live(rooted):
-                transpose_and_root(rooted, 0)
-            if live(quantised):
-                spread_sums(quantised)
-            if live(rooted):
-                transpose_and_root(rooted, 1)
-            if live(multiplied):
-                multiply(multiplied)
-            if live(rooted):
                 sum_rows(rooted, 0)
             if live(quantised):
                 quantise_half(quantised, 0)
@@ -314,14 +332,33 @@ def tile_probprotoseghead_w_e_kernel(
             if live(quantised):
                 quantise_half(quantised, 1)
             if live(rooted):
+                transpose_and_root(rooted, 0)
+            if live(quantised):
+                spread_sums(quantised)
+            if live(rooted):
+                transpose_and_root(rooted, 1)
+            if step == 0:
+                transpose_xv_and_root()
+                sum_rows(rooted, 2)
+                sum_rows(rooted, 3)
+                sum_xv()
+                quantise_xv()
+                make_pixel_term()
+            if step == 1:
+                transpose_x_and_copy()
+            for group in due:
+                multiply(group)
+            if live(rooted) and step > 0:
                 sum_rows(rooted, 2)
             if live(quantised):
                 make_shift(quantised)
-            if live(rooted):
+            if live(rooted) and step > 0:
                 sum_rows(rooted, 3)
-            if live(multiplied):
-                finish(multiplied)
+            if step == 1:
+                quantise_x()
             if live(step + ROW_GROUPS):
                 load_rows(step + ROW_GROUPS)
-            if live(step + ROW_GROUPS - 1):
-                load_words(step + ROW_GROUPS - 1)
+            if live(step + 2):
+                load_words(step + 2)
+            for group in due:
+                finish(group)

@@ -27,7 +27,7 @@ PAIR = 2 * P
 PAIRS = GROUP // PAIR
 LAM = 1.0 / D
 ROW_GROUPS = 4
-WORD_GROUPS = 6
+WORD_GROUPS = 5
 
 MULTIPLIED_IN_STEP = ((), (), (), (0,), (1,), (2, 3), (4,), (5, 6), (7,))
 
@@ -297,7 +297,7 @@ def tile_probprotoseghead_w_e_kernel(
             acc_of[group] = acc
 
         def finish(group):
-            result = work.tile([P, GROUP], F32, name="result")
+            result = work.tile([P, GROUP], F32, name="result", bufs=6)
             nc.vector.scalar_tensor_tensor(
                 out=result[:],
                 in0=acc_of[group][:],
@@ -342,7 +342,6 @@ def tile_probprotoseghead_w_e_kernel(
                 sum_rows(rooted, 2)
                 sum_rows(rooted, 3)
                 sum_xv()
-                quantise_xv()
                 make_pixel_term()
             if step == 1:
                 transpose_x_and_copy()
@@ -355,10 +354,11 @@ def tile_probprotoseghead_w_e_kernel(
             if live(rooted) and step > 0:
                 sum_rows(rooted, 3)
             if step == 1:
+                quantise_xv()
                 quantise_x()
+            for group in due:
+                finish(group)
             if live(step + ROW_GROUPS):
                 load_rows(step + ROW_GROUPS)
             if live(step + 2):
                 load_words(step + 2)
-            for group in due:
-                finish(group)

@@ -29,7 +29,8 @@ LAM = 1.0 / D
 ROW_GROUPS = 4
 WORD_GROUPS = 5
 
-MULTIPLIED_IN_STEP = ((), (), (), (0,), (1,), (2, 3), (4,), (5, 6), (7,))
+MULTIPLIED_IN_STEP = ((), (), (), (0,), (1,), (2, 3), (4, 5), (6,))
+SUMS_IN_STEP = (6, 4, 4, 5, 4, 4, 4, 1)
 
 FLOPS = 2 * 2 * P * CLASSES * PER_CLASS * D
 
@@ -308,56 +309,117 @@ def tile_probprotoseghead_w_e_kernel(
             )
             nc.sync.dma_start(out=out_cols[:, group * GROUP : (group + 1) * GROUP], in_=result[:])
 
-        for step in range(N_GROUPS + 1):
+        def quantise_part(group, g, pair):
+            cols = slice(pair * PAIR, (pair + 1) * PAIR)
+            quantise(
+                grouped_of[group][:, g, cols, :].rearrange("p c t -> p (c t)"),
+                codes_of[group][:, g, cols],
+                planes_of[group][:, g, cols],
+            )
+
+        def multiply_pair(group, pair):
+            acc = acc_pool.tile([P, GROUP], F32, name="acc")
+            here = slice(pair * PAIR, (pair + 1) * PAIR)
+            cols = slice(group * GROUP + pair * PAIR, group * GROUP + (pair + 1) * PAIR)
+            for g in range(PASSES):
+                nc.tensor.matmul_mx(
+                    out=acc[:, :PAIR],
+                    lhsT=x_codes[:, g, :].bitcast(FP8X4),
+                    lhsT_scale=x_planes[:, g, :],
+                    rhs=words_of[group][:, g, here].bitcast(FP8X4),
+                    rhs_scale=proto_planes[4 * g : P, cols],
+                    start=(g == 0),
+                    stop=False,
+                )
+            for g in range(PASSES):
+                nc.tensor.matmul_mx(
+                    out=acc[:, :PAIR],
+                    lhsT=xv_codes[:, g, :].bitcast(FP8X4),
+                    lhsT_scale=xv_planes[:, g, :],
+                    rhs=codes_of[group][:, g, here].bitcast(FP8X4),
+                    rhs_scale=planes_of[group][:, g, here],
+                    start=False,
+                    stop=(g == PASSES - 1),
+                )
+            acc_of[(group, pair)] = acc
+
+        def finish_pair(group, pair):
+            result = work.tile([P, GROUP], F32, name="result", bufs=6)
+            first = group * GROUP + pair * PAIR
+            nc.vector.scalar_tensor_tensor(
+                out=result[:, :PAIR],
+                in0=acc_of[(group, pair)][:, :PAIR],
+                scalar=2.0,
+                in1=shift_of[group][:, pair * PAIR : (pair + 1) * PAIR],
+                op0=ALU.mult,
+                op1=ALU.subtract,
+            )
+            nc.sync.dma_start(out=out_cols[:, first : first + PAIR], in_=result[:, :PAIR])
+
+        tiles = [(group, t) for group in range(N_GROUPS) for t in range(GROUP // P)]
+        summed = 0
+
+        def sum_next(count):
+            for group, t in tiles[summed : summed + count]:
+                if group not in sums_of:
+                    sums_of[group] = work.tile([P, GROUP // P], F32, name="sums", bufs=3)
+                sum_rows(group, t)
+            return summed + count
+
+        def new_codes(group):
+            codes_of[group] = codes_pool.tile([P, PASSES, GROUP], U32, name="codes", align_bytes=64)
+            planes_of[group] = codes_pool.tile([P, PASSES, GROUP], U8, name="planes", align_bytes=64)
+
+        for step in range(N_GROUPS):
             rooted, quantised = step, step - 1
+            last = step == N_GROUPS - 1
             due = MULTIPLIED_IN_STEP[step]
-            if live(rooted):
-                grouped_of[rooted] = grouped_pool.tile(
-                    [P, PASSES, GROUP, PACK], BF16, name="grouped", align_bytes=64
-                )
-                sums_of[rooted] = work.tile([P, GROUP // P], F32, name="sums")
+            sums_left = SUMS_IN_STEP[step]
+            grouped_of[rooted] = grouped_pool.tile(
+                [P, PASSES, GROUP, PACK], BF16, name="grouped", align_bytes=64
+            )
             if live(quantised):
-                codes_of[quantised] = codes_pool.tile(
-                    [P, PASSES, GROUP], U32, name="codes", align_bytes=64
-                )
-                planes_of[quantised] = codes_pool.tile(
-                    [P, PASSES, GROUP], U8, name="planes", align_bytes=64
-                )
-            if live(rooted):
-                sum_rows(rooted, 0)
-            if live(quantised):
-                quantise_half(quantised, 0)
-            if live(rooted):
-                sum_rows(rooted, 1)
-            if live(quantised):
-                quantise_half(quantised, 1)
-            if live(rooted):
-                transpose_and_root(rooted, 0)
+                new_codes(quantised)
+                for half in range(2):
+                    quantise_half(quantised, half)
+                    if sums_left:
+                        summed = sum_next(1)
+                        sums_left -= 1
+            transpose_and_root(rooted, 0)
             if live(quantised):
                 spread_sums(quantised)
-            if live(rooted):
-                transpose_and_root(rooted, 1)
+            transpose_and_root(rooted, 1)
             if step == 0:
                 transpose_xv_and_root()
-                sum_rows(rooted, 2)
-                sum_rows(rooted, 3)
+                summed = sum_next(4)
+                sums_left -= 4
                 sum_xv()
                 make_pixel_term()
             if step == 1:
                 transpose_x_and_copy()
             for group in due:
                 multiply(group)
-            if live(rooted) and step > 0:
-                sum_rows(rooted, 2)
+            summed = sum_next(sums_left)
             if live(quantised):
                 make_shift(quantised)
-            if live(rooted) and step > 0:
-                sum_rows(rooted, 3)
             if step == 1:
                 quantise_xv()
                 quantise_x()
+            if last:
+                new_codes(rooted)
+                for g in range(PASSES):
+                    quantise_part(rooted, g, 0)
+                spread_sums(rooted)
+                multiply_pair(rooted, 0)
             for group in due:
                 finish(group)
+            if last:
+                make_shift(rooted)
+                finish_pair(rooted, 0)
+                for g in range(PASSES):
+                    quantise_part(rooted, g, 1)
+                multiply_pair(rooted, 1)
+                finish_pair(rooted, 1)
             if live(step + ROW_GROUPS):
                 load_rows(step + ROW_GROUPS)
             if live(step + 2):

@@ -29,7 +29,6 @@ LAM = 1.0 / D
 ROW_GROUPS = 4
 WORD_GROUPS = 5
 
-MULTIPLIED_IN_STEP = ((), (), (), (0,), (1,), (2, 3), (4, 5), (6,))
 SUMS_IN_STEP = (6, 4, 4, 5, 4, 4, 4, 1)
 
 FLOPS = 2 * 2 * P * CLASSES * PER_CLASS * D
@@ -51,8 +50,8 @@ def tile_probprotoseghead_w_e_kernel(
         grouped_pool = stack.enter_context(tc.tile_pool(name="grouped", bufs=2))
         codes_pool = stack.enter_context(tc.tile_pool(name="codes", bufs=3))
         work = stack.enter_context(tc.tile_pool(name="work", bufs=2))
-        banks = stack.enter_context(tc.psum_pool(name="banks", bufs=5))
-        acc_pool = stack.enter_context(tc.psum_pool(name="acc", bufs=2))
+        banks = stack.enter_context(tc.psum_pool(name="banks", bufs=4))
+        acc_pool = stack.enter_context(tc.psum_pool(name="acc", bufs=3))
         spread_pool = stack.enter_context(tc.psum_pool(name="spread", bufs=1))
         stack.enter_context(tc.manual_schedule())
 
@@ -224,19 +223,18 @@ def tile_probprotoseghead_w_e_kernel(
         shift_of = {}
         acc_of = {}
 
-        def transpose_and_root(group, pair):
+        def transpose_and_root(group, pair, g):
             rows = rows_of[(group, pair)]
-            for g in range(PASSES):
-                bank = banks.tile([P, GROUP], F32, name="bank")
-                transpose_four(
-                    bank,
-                    [
-                        rows[:, t, :].bitcast(F32)[:, (2 * g + u) * P : (2 * g + u + 1) * P]
-                        for u in range(2)
-                        for t in range(2)
-                    ],
-                )
-                root(bank, grouped_of[group][:, g, pair * PAIR : (pair + 1) * PAIR, :], 1.0)
+            bank = banks.tile([P, GROUP], F32, name="bank")
+            transpose_four(
+                bank,
+                [
+                    rows[:, t, :].bitcast(F32)[:, (2 * g + u) * P : (2 * g + u + 1) * P]
+                    for u in range(2)
+                    for t in range(2)
+                ],
+            )
+            root(bank, grouped_of[group][:, g, pair * PAIR : (pair + 1) * PAIR, :], 1.0)
 
         def sum_rows(group, tile_index):
             rows = rows_of[(group, tile_index // 2)]
@@ -250,15 +248,16 @@ def tile_probprotoseghead_w_e_kernel(
                 planes_of[group][:, passes, :].rearrange("p g c -> p (g c)"),
             )
 
-        def spread_sums(group):
-            spread = spread_pool.tile([P, GROUP], F32, name="spread")
-            for t in range(GROUP // P):
-                nc.tensor.transpose(
-                    spread[:, t * P : (t + 1) * P],
-                    sums_of[group][:, t : t + 1].to_broadcast([P, P]),
-                    ident[:],
-                )
-            spread_of[group] = spread
+        def spread_sums(group, t):
+            if t == 0:
+                spread_of[group] = spread_pool.tile([P, GROUP], F32, name="spread")
+            nc.tensor.matmul(
+                spread_of[group][:, t * P : (t + 1) * P],
+                lhsT=sums_of[group][:, t : t + 1].to_broadcast([P, P]),
+                rhs=ident[:],
+                start=True,
+                stop=True,
+            )
 
         def make_shift(group):
             shift = work.tile([P, GROUP], F32, name="shift", bufs=4)
@@ -272,30 +271,43 @@ def tile_probprotoseghead_w_e_kernel(
             )
             shift_of[group] = shift
 
-        def multiply(group):
-            acc = acc_pool.tile([P, GROUP], F32, name="acc")
-            cols = slice(group * GROUP, (group + 1) * GROUP)
-            for g in range(PASSES):
-                nc.tensor.matmul_mx(
-                    out=acc[:],
-                    lhsT=xv_codes[:, g, :].bitcast(FP8X4),
-                    lhsT_scale=xv_planes[:, g, :],
-                    rhs=codes_of[group][:, g, :].bitcast(FP8X4),
-                    rhs_scale=planes_of[group][:, g, :],
-                    start=(g == 0),
-                    stop=False,
+        def cross_pass(acc, group, g, here, start, stop):
+            nc.tensor.matmul_mx(
+                out=acc,
+                lhsT=xv_codes[:, g, :].bitcast(FP8X4),
+                lhsT_scale=xv_planes[:, g, :],
+                rhs=codes_of[group][:, g, here].bitcast(FP8X4),
+                rhs_scale=planes_of[group][:, g, here],
+                start=start,
+                stop=stop,
+            )
+
+        def dot_pass(acc, group, g, here, start, stop):
+            nc.tensor.matmul_mx(
+                out=acc,
+                lhsT=x_codes[:, g, :].bitcast(FP8X4),
+                lhsT_scale=x_planes[:, g, :],
+                rhs=words_of[group][:, g, here].bitcast(FP8X4),
+                rhs_scale=proto_planes[
+                    4 * g : P, group * GROUP + here.start : group * GROUP + here.stop
+                ],
+                start=start,
+                stop=stop,
+            )
+
+        def multiply(group, numbers):
+            for number in numbers:
+                if number == 0:
+                    acc_of[group] = acc_pool.tile([P, GROUP], F32, name="acc")
+                one_pass = cross_pass if number < PASSES else dot_pass
+                one_pass(
+                    acc_of[group][:],
+                    group,
+                    number % PASSES,
+                    slice(0, GROUP),
+                    start=(number == 0),
+                    stop=(number == 2 * PASSES - 1),
                 )
-            for g in range(PASSES):
-                nc.tensor.matmul_mx(
-                    out=acc[:],
-                    lhsT=x_codes[:, g, :].bitcast(FP8X4),
-                    lhsT_scale=x_planes[:, g, :],
-                    rhs=words_of[group][:, g, :].bitcast(FP8X4),
-                    rhs_scale=proto_planes[4 * g : P, cols],
-                    start=False,
-                    stop=(g == PASSES - 1),
-                )
-            acc_of[group] = acc
 
         def finish(group):
             result = work.tile([P, GROUP], F32, name="result", bufs=6)
@@ -316,32 +328,6 @@ def tile_probprotoseghead_w_e_kernel(
                 codes_of[group][:, g, cols],
                 planes_of[group][:, g, cols],
             )
-
-        def multiply_pair(group, pair):
-            acc = acc_pool.tile([P, GROUP], F32, name="acc")
-            here = slice(pair * PAIR, (pair + 1) * PAIR)
-            cols = slice(group * GROUP + pair * PAIR, group * GROUP + (pair + 1) * PAIR)
-            for g in range(PASSES):
-                nc.tensor.matmul_mx(
-                    out=acc[:, :PAIR],
-                    lhsT=x_codes[:, g, :].bitcast(FP8X4),
-                    lhsT_scale=x_planes[:, g, :],
-                    rhs=words_of[group][:, g, here].bitcast(FP8X4),
-                    rhs_scale=proto_planes[4 * g : P, cols],
-                    start=(g == 0),
-                    stop=False,
-                )
-            for g in range(PASSES):
-                nc.tensor.matmul_mx(
-                    out=acc[:, :PAIR],
-                    lhsT=xv_codes[:, g, :].bitcast(FP8X4),
-                    lhsT_scale=xv_planes[:, g, :],
-                    rhs=codes_of[group][:, g, here].bitcast(FP8X4),
-                    rhs_scale=planes_of[group][:, g, here],
-                    start=False,
-                    stop=(g == PASSES - 1),
-                )
-            acc_of[(group, pair)] = acc
 
         def finish_pair(group, pair):
             result = work.tile([P, GROUP], F32, name="result", bufs=6)
@@ -371,9 +357,8 @@ def tile_probprotoseghead_w_e_kernel(
             planes_of[group] = codes_pool.tile([P, PASSES, GROUP], U8, name="planes", align_bytes=64)
 
         for step in range(N_GROUPS):
-            rooted, quantised = step, step - 1
+            rooted, quantised, multiplied = step, step - 1, step - 3
             last = step == N_GROUPS - 1
-            due = MULTIPLIED_IN_STEP[step]
             sums_left = SUMS_IN_STEP[step]
             grouped_of[rooted] = grouped_pool.tile(
                 [P, PASSES, GROUP, PACK], BF16, name="grouped", align_bytes=64
@@ -385,10 +370,16 @@ def tile_probprotoseghead_w_e_kernel(
                     if sums_left:
                         summed = sum_next(1)
                         sums_left -= 1
-            transpose_and_root(rooted, 0)
-            if live(quantised):
-                spread_sums(quantised)
-            transpose_and_root(rooted, 1)
+            for quarter in range(4):
+                for g in (2 * (quarter % 2), 2 * (quarter % 2) + 1):
+                    transpose_and_root(rooted, quarter // 2, g)
+                if live(quantised) and quarter >= 2:
+                    spread_sums(quantised, 2 * quarter - 4)
+                    spread_sums(quantised, 2 * quarter - 3)
+                if live(multiplied):
+                    multiply(multiplied, (2 * quarter, 2 * quarter + 1))
+                if last:
+                    multiply(rooted - 2 + quarter // 2, (2 * (quarter % 2), 2 * (quarter % 2) + 1))
             if step == 0:
                 transpose_xv_and_root()
                 summed = sum_next(4)
@@ -397,30 +388,46 @@ def tile_probprotoseghead_w_e_kernel(
                 make_pixel_term()
             if step == 1:
                 transpose_x_and_copy()
-            for group in due:
-                multiply(group)
             summed = sum_next(sums_left)
             if live(quantised):
                 make_shift(quantised)
             if step == 1:
                 quantise_xv()
                 quantise_x()
-            if last:
-                new_codes(rooted)
-                for g in range(PASSES):
-                    quantise_part(rooted, g, 0)
-                spread_sums(rooted)
-                multiply_pair(rooted, 0)
-            for group in due:
-                finish(group)
-            if last:
-                make_shift(rooted)
-                finish_pair(rooted, 0)
-                for g in range(PASSES):
-                    quantise_part(rooted, g, 1)
-                multiply_pair(rooted, 1)
-                finish_pair(rooted, 1)
+            if live(multiplied):
+                finish(multiplied)
             if live(step + ROW_GROUPS):
                 load_rows(step + ROW_GROUPS)
             if live(step + 2):
                 load_words(step + 2)
+
+        final = N_GROUPS - 1
+        halves = [slice(pair * PAIR, (pair + 1) * PAIR) for pair in range(PAIRS)]
+        new_codes(final)
+        for g in range(PASSES):
+            quantise_part(final, g, 0)
+        for group in (final - 2, final - 1):
+            multiply(group, range(PASSES, 2 * PASSES))
+            finish(group)
+        for t in range(GROUP // P):
+            spread_sums(final, t)
+        make_shift(final)
+        for pair in range(PAIRS):
+            acc_of[(final, pair)] = acc_pool.tile([P, GROUP], F32, name="acc")
+        for g in range(PASSES):
+            for pair, here in enumerate(halves):
+                dot_pass(acc_of[(final, pair)][:, :PAIR], final, g, here, start=(g == 0), stop=False)
+        for pair, here in enumerate(halves):
+            for g in range(PASSES):
+                if pair == 1:
+                    quantise_part(final, g, 1)
+                cross_pass(
+                    acc_of[(final, pair)][:, :PAIR],
+                    final,
+                    g,
+                    here,
+                    start=False,
+                    stop=(g == PASSES - 1),
+                )
+        for pair in range(PAIRS):
+            finish_pair(final, pair)

@@ -62,6 +62,13 @@ def tile_probprotoseghead_w_e_kernel(
             for slot, block in enumerate(blocks):
                 nc.tensor.transpose(bank[:, slot * P : (slot + 1) * P], block, ident[:])
 
+        def root_rows(bank, dest):
+            nc.scalar.activation(
+                out=dest.rearrange("p c q -> p (c q)").rearrange("p (r s e) -> p r s e", s=4, e=2),
+                in_=bank[:].bitcast(BF16).rearrange("p (s r e) -> p r s e", s=4, e=2),
+                func=SQRT,
+            )
+
         def root(bank, dest, scale):
             nc.scalar.activation(
                 out=dest.rearrange("p c (u e) -> p c u e", u=2),
@@ -91,7 +98,7 @@ def tile_probprotoseghead_w_e_kernel(
         def load_pair(group, pair, pieces=1):
             rows = rows_pool.tile([P, 2, D], BF16, name="rows")
             first = group * GROUP + pair * PAIR
-            source = var_rows[first : first + PAIR, :].rearrange("(t p) d -> p t d", p=P)
+            source = var_rows[first : first + PAIR, :].rearrange("(p t) d -> p t d", p=P)
             for piece in range(pieces):
                 cols = slice(piece * D // pieces, (piece + 1) * D // pieces)
                 nc.sync.dma_start(out=rows[:, :, cols], in_=source[:, :, cols])
@@ -230,11 +237,11 @@ def tile_probprotoseghead_w_e_kernel(
                 bank,
                 [
                     rows[:, t, :].bitcast(F32)[:, (2 * g + u) * P : (2 * g + u + 1) * P]
-                    for u in range(2)
                     for t in range(2)
+                    for u in range(2)
                 ],
             )
-            root(bank, grouped_of[group][:, g, pair * PAIR : (pair + 1) * PAIR, :], 1.0)
+            root_rows(bank, grouped_of[group][:, g, pair * PAIR : (pair + 1) * PAIR, :])
 
         def sum_rows(group, tile_index):
             rows = rows_of[(group, tile_index // 2)]
@@ -262,8 +269,8 @@ def tile_probprotoseghead_w_e_kernel(
         def make_shift(group):
             shift = work.tile([P, GROUP], F32, name="shift", bufs=4)
             nc.vector.tensor_scalar(
-                out=shift[:],
-                in0=spread_of[group][:],
+                out=shift[:].rearrange("p (a r t) -> p a r t", a=PAIRS, t=2),
+                in0=spread_of[group][:].rearrange("p (a t r) -> p a r t", a=PAIRS, t=2),
                 scalar1=LAM,
                 scalar2=pixel_term[:, 0:1],
                 op0=ALU.mult,

@@ -20,18 +20,18 @@ PASSES = D // K_PASS
 BLOCKS = D // 32
 CLASSES = 64
 PER_CLASS = 64
+N_PROTO = CLASSES * PER_CLASS
+UNIT = 2 * P
+N_UNITS = N_PROTO // UNIT
 GROUP = 512
-N_GROUPS = CLASSES * PER_CLASS // GROUP
+N_GROUPS = N_PROTO // GROUP
 GROUP_CLASSES = GROUP // PER_CLASS
-PAIR = 2 * P
-PAIRS = GROUP // PAIR
+UNIT_PASSES = 10
+FIRST = 13
+LEFT = 4
 LAM = 1.0 / D
-ROW_GROUPS = 4
-WORD_GROUPS = 5
 
-SUMS_IN_STEP = (6, 4, 4, 5, 4, 4, 4, 1)
-
-FLOPS = 2 * 2 * P * CLASSES * PER_CLASS * D
+FLOPS = 2 * 2 * P * N_PROTO * D
 
 
 def tile_probprotoseghead_w_e_kernel(
@@ -39,124 +39,162 @@ def tile_probprotoseghead_w_e_kernel(
 ):
     nc = tc.nc
     var_rows = proto_var.rearrange("c m d -> (c m) d")
+    run_view = prototypes_words.rearrange("(c g) p m t -> c (g p m t)", g=PASSES).rearrange(
+        "c (a q b) -> a q c b", a=2, q=P
+    )[0]
     word_view = prototypes_words.rearrange("(c g) p m t -> g p c (m t)", g=PASSES)
     scale_view = prototypes_scales.rearrange("(c g) q m -> (g q) c m", g=PASSES)
     out_cols = out.rearrange("n c m -> n (c m)")
 
     with ExitStack() as stack:
         const = stack.enter_context(tc.tile_pool(name="const", bufs=1))
-        rows_pool = stack.enter_context(tc.tile_pool(name="rows", bufs=ROW_GROUPS * PAIRS))
-        words_pool = stack.enter_context(tc.tile_pool(name="words", bufs=WORD_GROUPS))
+        rows_pool = stack.enter_context(tc.tile_pool(name="rows", bufs=7))
+        raw_pool = stack.enter_context(tc.tile_pool(name="raw", bufs=3))
+        words_pool = stack.enter_context(tc.tile_pool(name="words", bufs=3))
         grouped_pool = stack.enter_context(tc.tile_pool(name="grouped", bufs=2))
-        codes_pool = stack.enter_context(tc.tile_pool(name="codes", bufs=3))
+        codes_pool = stack.enter_context(tc.tile_pool(name="codes", bufs=6))
         work = stack.enter_context(tc.tile_pool(name="work", bufs=2))
         banks = stack.enter_context(tc.psum_pool(name="banks", bufs=4))
         acc_pool = stack.enter_context(tc.psum_pool(name="acc", bufs=3))
         spread_pool = stack.enter_context(tc.psum_pool(name="spread", bufs=1))
         stack.enter_context(tc.manual_schedule())
 
-        def live(group):
-            return 0 <= group < N_GROUPS
-
         def transpose_four(bank, blocks):
             for slot, block in enumerate(blocks):
                 nc.tensor.transpose(bank[:, slot * P : (slot + 1) * P], block, ident[:])
 
-        def root_rows(bank, dest):
-            nc.scalar.activation(
-                out=dest.rearrange("p c q -> p (c q)").rearrange("p (r s e) -> p r s e", s=4, e=2),
-                in_=bank[:].bitcast(BF16).rearrange("p (s r e) -> p r s e", s=4, e=2),
-                func=SQRT,
-            )
+        def quantise(grouped, codes, planes):
+            nc.vector.quantize_mx(out=codes.bitcast(FP8X4), scales=planes, in_=grouped)
 
-        def root(bank, dest, scale):
-            nc.scalar.activation(
-                out=dest.rearrange("p c (u e) -> p c u e", u=2),
-                in_=bank[:].bitcast(BF16).rearrange("p (u c e) -> p c u e", u=2, e=2),
-                func=SQRT,
-                scale=scale,
-            )
-
-        def sum_row(row, total):
-            junk = work.tile([P, D // 2], F32, name="junk")
+        def sum_row(first_half, second_half, total):
+            junk = work.tile([P, 2, D // 4], F32, name="junk")
             nc.vector.scalar_tensor_tensor(
                 out=junk[:],
-                in0=row[:, : D // 2],
+                in0=first_half,
                 scalar=1.0,
-                in1=row[:, D // 2 :],
+                in1=second_half,
                 op0=ALU.mult,
                 op1=ALU.add,
                 accum_out=total,
             )
 
-        def quantise(grouped, codes, planes):
-            nc.vector.quantize_mx(out=codes.bitcast(FP8X4), scales=planes, in_=grouped)
-
         rows_of = {}
+        raw_of = {}
         words_of = {}
 
-        def load_pair(group, pair, pieces=1):
-            rows = rows_pool.tile([P, 2, D], BF16, name="rows")
-            first = group * GROUP + pair * PAIR
-            source = var_rows[first : first + PAIR, :].rearrange("(p t) d -> p t d", p=P)
-            for piece in range(pieces):
-                cols = slice(piece * D // pieces, (piece + 1) * D // pieces)
-                nc.sync.dma_start(out=rows[:, :, cols], in_=source[:, :, cols])
-            rows_of[(group, pair)] = rows
+        def source_of(unit):
+            return var_rows[unit * UNIT : (unit + 1) * UNIT, :].rearrange("(p t) d -> p t d", t=2)
 
-        def load_rows(group):
-            for pair in range(PAIRS):
-                load_pair(group, pair)
-
-        def load_words(group):
-            words = words_pool.tile([P, PASSES, GROUP], U32, name="words", align_bytes=64)
-            first = group * GROUP_CLASSES
+        def load_first_rows():
+            rows = const.tile([P, PASSES, 2, K_PASS], BF16, name="first_rows")
             for g in range(PASSES):
                 nc.sync.dma_start(
-                    out=words[:, g, :].bitcast(I32).rearrange("p (c w) -> p c w", c=GROUP_CLASSES),
-                    in_=word_view[g][:, first : first + GROUP_CLASSES, :].bitcast(I32),
+                    out=rows[:, g, :, :], in_=source_of(0)[:, :, g * K_PASS : (g + 1) * K_PASS]
+                )
+            rows_of[0] = rows[:]
+
+        def load_rows(unit):
+            rows = rows_pool.tile([P, 2, D], BF16, name="rows")
+            nc.sync.dma_start(out=rows[:], in_=source_of(unit))
+            rows_of[unit] = rows[:].rearrange("p t (g k) -> p g t k", g=PASSES)
+
+        def load_words(group):
+            classes = slice(group * GROUP_CLASSES, (group + 1) * GROUP_CLASSES)
+            raw = raw_pool.tile([P, GROUP_CLASSES, 2 * PER_CLASS], U32, name="raw", align_bytes=64)
+            nc.sync.dma_start(out=raw[:].bitcast(I32), in_=run_view[:, classes, :].bitcast(I32))
+            raw_of[group] = raw
+            words = words_pool.tile([P, 4, GROUP_CLASSES, PER_CLASS], U32, name="words", align_bytes=64)
+            for g in (2, 3):
+                nc.sync.dma_start(
+                    out=words[:, g].bitcast(I32), in_=word_view[g][:, classes, :].bitcast(I32)
                 )
             words_of[group] = words
 
-        proto_planes = const.tile([P, CLASSES * PER_CLASS], U8, name="proto_planes", align_bytes=64)
+        proto_planes = const.tile([P, N_PROTO], U8, name="proto_planes", align_bytes=64)
         nc.vector.memset(proto_planes[:].bitcast(I32), 0)
+        zeros = const.tile([P, 2, P], U32, name="zeros")
+        nc.gpsimd.memset(zeros[:].bitcast(I32), 0)
         ident = const.tile([P, P], F32, name="ident")
         make_identity(nc, ident[:])
 
-        load_pair(0, 0, pieces=PASSES)
-        load_pair(0, 1)
-        xv_rows = const.tile([P, D], BF16, name="xv_rows")
-        nc.sync.dma_start(out=xv_rows[:], in_=x_var)
-        load_pair(1, 0)
-        staged_scales = const.tile(
-            [BLOCKS, CLASSES * PER_CLASS], U8, name="staged_scales", align_bytes=64
-        )
+        load_first_rows()
+        load_rows(1)
+        x_rows = const.tile([P, D], BF16, name="x_rows")
+        nc.sync.dma_start(out=x_rows[:], in_=x)
+        staged_scales = const.tile([BLOCKS, N_PROTO], U8, name="staged_scales", align_bytes=64)
         nc.sync.dma_start(
             out=staged_scales[:].bitcast(I32).rearrange("b (c w) -> b c w", c=CLASSES),
             in_=scale_view.bitcast(I32),
         )
-        load_pair(1, 1)
-        x_rows = const.tile([P, D], BF16, name="x_rows")
-        nc.sync.dma_start(out=x_rows[:], in_=x)
+        xv_rows = const.tile([P, D], BF16, name="xv_rows")
+        nc.sync.dma_start(out=xv_rows[:], in_=x_var)
         load_rows(2)
-        for g in range(PASSES):
+        for plane in range(4):
             for r in range(4):
+                rows = slice(2 * r + plane, 32, 8) if plane < 2 else slice(16 * plane + r, 16 * plane + 16, 4)
                 nc.sync.dma_start(
-                    out=proto_planes[4 * g + r : P : 32, :].bitcast(I32),
-                    in_=staged_scales[16 * g + r : 16 * g + 16 : 4, :].bitcast(I32),
+                    out=proto_planes[4 * plane + r : P : 32, :].bitcast(I32),
+                    in_=staged_scales[rows, :].bitcast(I32),
                 )
-        load_words(0)
-        load_rows(3)
-        load_words(1)
+            load_rows(3 + plane)
 
+        xs = const.tile([P, 2, 2, 2, P], F32, name="xs")
         xv_grouped = const.tile([P, PASSES, P, PACK], BF16, name="xv_grouped", align_bytes=64)
-        x_grouped = const.tile([P, PASSES, P, PACK], BF16, name="x_grouped", align_bytes=64)
+        x_grouped = const.tile([P, 6, P, PACK], BF16, name="x_grouped", align_bytes=64)
         xv_codes = const.tile([P, PASSES, P], U32, name="xv_codes", align_bytes=64)
-        x_codes = const.tile([P, PASSES, P], U32, name="x_codes", align_bytes=64)
+        x_codes = const.tile([P, 6, P], U32, name="x_codes", align_bytes=64)
         xv_planes = const.tile([P, PASSES, P], U8, name="xv_planes", align_bytes=64)
-        x_planes = const.tile([P, PASSES, P], U8, name="x_planes", align_bytes=64)
+        x_planes = const.tile([P, 6, P], U8, name="x_planes", align_bytes=64)
         xv_sum = const.tile([P, 1], F32, name="xv_sum")
         pixel_term = const.tile([P, 1], F32, name="pixel_term")
+
+        def sort_x():
+            source = x_rows[:, : D // 2].bitcast(F32).rearrange("p (c v i j u) -> p v j u c i", c=16, v=2, i=4, j=2)
+            dest = xs[:].rearrange("p v s u (c j i) -> p v s j u c i", j=2, i=4)
+            for ab in range(2):
+                for sw in range(2):
+                    for jj in range(2):
+                        nc.vector.tensor_copy(out=dest[:, ab, sw, jj], in_=source[:, ab, (jj + sw) % 2])
+
+        x_banks = {}
+
+        def transpose_x(b):
+            bank = banks.tile([P, GROUP], F32, name="bank")
+            x_words = x_rows[:].bitcast(F32)
+            transpose_four(
+                bank,
+                [
+                    xs[:, b, v, u, :] if b < 2 else x_words[:, 2 * P * (2 + v) + u : 2 * P * (3 + v) : 2]
+                    for u in range(2)
+                    for v in range(2)
+                ],
+            )
+            x_banks[b] = bank
+
+        def copy_x(b):
+            nc.vector.tensor_copy(
+                out=x_grouped[:, 2 * b : 2 * b + 2, :, :]
+                .bitcast(F32)
+                .rearrange("p g n u -> p (g n) u"),
+                in_=x_banks[b][:].rearrange("p (u c) -> p c u", u=2),
+            )
+
+        def quantise_x():
+            for tiles in (slice(0, 4), slice(4, 6)):
+                quantise(
+                    x_grouped[:, tiles].rearrange("p g n t -> p (g n t)"),
+                    x_codes[:, tiles].rearrange("p g n -> p (g n)"),
+                    x_planes[:, tiles].rearrange("p g n -> p (g n)"),
+                )
+
+        def zero_other_halves():
+            for ab in range(2):
+                for i in range(4):
+                    start = 4 * (1 - ab) + i
+                    nc.sync.dma_start(
+                        out=x_codes[start : P : 8, 2 * ab : 2 * ab + 2, :].bitcast(I32),
+                        in_=zeros[start : P : 8, :, :].bitcast(I32),
+                    )
 
         def transpose_xv_and_root():
             xv_words = xv_rows[:].bitcast(F32)
@@ -170,43 +208,14 @@ def tile_probprotoseghead_w_e_kernel(
                         for g in (2 * half, 2 * half + 1)
                     ],
                 )
-                root(
-                    bank,
-                    xv_grouped[:, 2 * half : 2 * half + 2, :, :].rearrange("p g n t -> p (g n) t"),
-                    LAM * LAM,
+                nc.scalar.activation(
+                    out=xv_grouped[:, 2 * half : 2 * half + 2, :, :].rearrange(
+                        "p g n (u e) -> p (g n) u e", u=2
+                    ),
+                    in_=bank[:].bitcast(BF16).rearrange("p (u c e) -> p c u e", u=2, e=2),
+                    func=SQRT,
+                    scale=LAM * LAM,
                 )
-
-        def transpose_x_and_copy():
-            x_words = x_rows[:].bitcast(F32)
-            for half in range(2):
-                bank = banks.tile([P, GROUP], F32, name="bank")
-                transpose_four(
-                    bank,
-                    [
-                        x_words[:, 2 * P * g + u : 2 * P * (g + 1) : 2]
-                        for u in range(2)
-                        for g in (2 * half, 2 * half + 1)
-                    ],
-                )
-                nc.vector.tensor_copy(
-                    out=x_grouped[:, 2 * half : 2 * half + 2, :, :]
-                    .bitcast(F32)
-                    .rearrange("p g n u -> p (g n) u"),
-                    in_=bank[:].rearrange("p (u c) -> p c u", u=2),
-                )
-
-        def sum_xv():
-            sum_row(xv_rows, xv_sum[:])
-
-        def make_pixel_term():
-            nc.vector.tensor_scalar(
-                out=pixel_term[:],
-                in0=xv_sum[:],
-                scalar1=LAM,
-                scalar2=2.0,
-                op0=ALU.mult,
-                op1=ALU.add,
-            )
 
         def quantise_xv():
             quantise(
@@ -215,11 +224,19 @@ def tile_probprotoseghead_w_e_kernel(
                 xv_planes[:].rearrange("p g n -> p (g n)"),
             )
 
-        def quantise_x():
-            quantise(
-                x_grouped[:].rearrange("p g n t -> p (g n t)"),
-                x_codes[:].rearrange("p g n -> p (g n)"),
-                x_planes[:].rearrange("p g n -> p (g n)"),
+        def make_pixel_term():
+            sum_row(
+                xv_rows[:, : D // 2].rearrange("p (h k) -> p h k", h=2),
+                xv_rows[:, D // 2 :].rearrange("p (h k) -> p h k", h=2),
+                xv_sum[:],
+            )
+            nc.vector.tensor_scalar(
+                out=pixel_term[:],
+                in0=xv_sum[:],
+                scalar1=LAM,
+                scalar2=2.0,
+                op0=ALU.mult,
+                op1=ALU.add,
             )
 
         grouped_of = {}
@@ -230,47 +247,80 @@ def tile_probprotoseghead_w_e_kernel(
         shift_of = {}
         acc_of = {}
 
-        def transpose_and_root(group, pair, g):
-            rows = rows_of[(group, pair)]
+        def transpose_and_root(unit, g):
+            if g == 0:
+                grouped_of[unit] = grouped_pool.tile(
+                    [P, PASSES, UNIT, PACK], BF16, name="grouped", align_bytes=64
+                )
             bank = banks.tile([P, GROUP], F32, name="bank")
             transpose_four(
                 bank,
                 [
-                    rows[:, t, :].bitcast(F32)[:, (2 * g + u) * P : (2 * g + u + 1) * P]
+                    rows_of[unit][:, g, t, :].bitcast(F32)[:, u * P : (u + 1) * P]
                     for t in range(2)
                     for u in range(2)
                 ],
             )
-            root_rows(bank, grouped_of[group][:, g, pair * PAIR : (pair + 1) * PAIR, :])
+            nc.scalar.activation(
+                out=grouped_of[unit][:, g, :, :]
+                .rearrange("p c q -> p (c q)")
+                .rearrange("p (r s e) -> p r s e", s=4, e=2),
+                in_=bank[:].bitcast(BF16).rearrange("p (s r e) -> p r s e", s=4, e=2),
+                func=SQRT,
+            )
 
-        def sum_rows(group, tile_index):
-            rows = rows_of[(group, tile_index // 2)]
-            sum_row(rows[:, tile_index % 2, :], sums_of[group][:, tile_index : tile_index + 1])
+        def sum_tile(tile_index):
+            unit, t = tile_index // 2, tile_index % 2
+            group, column = tile_index // 4, tile_index % 4
+            if column == 0:
+                sums_of[group] = work.tile([P, 4], F32, name="sums", bufs=3)
+            sum_row(
+                rows_of[unit][:, 0:2, t, :],
+                rows_of[unit][:, 2:4, t, :],
+                sums_of[group][:, column : column + 1],
+            )
 
-        def quantise_half(group, half):
-            passes = slice(2 * half, 2 * half + 2)
+        def new_codes(unit):
+            codes_of[unit] = codes_pool.tile([P, PASSES, UNIT], U32, name="codes", align_bytes=64)
+            planes_of[unit] = codes_pool.tile([P, PASSES, UNIT], U8, name="planes", align_bytes=64)
+
+        def quantise_unit(unit):
+            new_codes(unit)
             quantise(
-                grouped_of[group][:, passes, :, :].rearrange("p g c t -> p (g c t)"),
-                codes_of[group][:, passes, :].rearrange("p g c -> p (g c)"),
-                planes_of[group][:, passes, :].rearrange("p g c -> p (g c)"),
+                grouped_of[unit][:].rearrange("p g c t -> p (g c t)"),
+                codes_of[unit][:].rearrange("p g c -> p (g c)"),
+                planes_of[unit][:].rearrange("p g c -> p (g c)"),
             )
 
-        def spread_sums(group, t):
-            if t == 0:
-                spread_of[group] = spread_pool.tile([P, GROUP], F32, name="spread")
-            nc.tensor.matmul(
-                spread_of[group][:, t * P : (t + 1) * P],
-                lhsT=sums_of[group][:, t : t + 1].to_broadcast([P, P]),
-                rhs=ident[:],
-                start=True,
-                stop=True,
+        def quantise_part(unit, g):
+            if g == 0:
+                new_codes(unit)
+            quantise(
+                grouped_of[unit][:, g, :, :].rearrange("p c t -> p (c t)"),
+                codes_of[unit][:, g, :],
+                planes_of[unit][:, g, :],
             )
+
+        def sort_words(group):
+            nc.vector.tensor_copy(
+                out=words_of[group][:, 0:2].bitcast(I32),
+                in_=raw_of[group][:].bitcast(I32).rearrange("p c (j m) -> p j c m", j=2),
+            )
+
+        def spread_sums(group):
+            spread_of[group] = spread_pool.tile([P, GROUP], F32, name="spread")
+            for column in range(4):
+                nc.tensor.transpose(
+                    spread_of[group][:, column * P : (column + 1) * P],
+                    sums_of[group][:, column : column + 1].to_broadcast([P, P]),
+                    ident[:],
+                )
 
         def make_shift(group):
             shift = work.tile([P, GROUP], F32, name="shift", bufs=4)
             nc.vector.tensor_scalar(
-                out=shift[:].rearrange("p (a r t) -> p a r t", a=PAIRS, t=2),
-                in0=spread_of[group][:].rearrange("p (a t r) -> p a r t", a=PAIRS, t=2),
+                out=shift[:].rearrange("p (a r t) -> p a r t", a=2, t=2),
+                in0=spread_of[group][:].rearrange("p (a t r) -> p a r t", a=2, t=2),
                 scalar1=LAM,
                 scalar2=pixel_term[:, 0:1],
                 op0=ALU.mult,
@@ -278,163 +328,145 @@ def tile_probprotoseghead_w_e_kernel(
             )
             shift_of[group] = shift
 
-        def cross_pass(acc, group, g, here, start, stop):
+        def accumulator(unit):
+            group, half = unit // 2, unit % 2
+            if group == N_GROUPS - 1:
+                if unit not in acc_of:
+                    acc_of[unit] = acc_pool.tile([P, GROUP], F32, name="acc")
+                return acc_of[unit][:, :UNIT]
+            if group not in acc_of:
+                acc_of[group] = acc_pool.tile([P, GROUP], F32, name="acc")
+            return acc_of[group][:, half * UNIT : (half + 1) * UNIT]
+
+        def order_of(unit):
+            return (4, 5, 6, 7, 0, 1, 2, 8, 9, 3) if unit == N_UNITS - 1 else tuple(range(UNIT_PASSES))
+
+        def multiply(unit, number):
+            group, first = unit // 2, unit % 2 * UNIT
+            column = group * GROUP + first
+            if number < 4:
+                left, left_plane = xv_codes[:, number, :], xv_planes[:, number, :]
+                right, right_plane = codes_of[unit][:, number, :], planes_of[unit][:, number, :]
+            else:
+                if number < 8:
+                    j, ab = number // 2 % 2, number % 2
+                    tile_index, which, plane = 2 * ab + (ab + j) % 2, j, ab
+                else:
+                    tile_index, which, plane = number - 4, number - 6, number - 6
+                left, left_plane = x_codes[:, tile_index, :], x_planes[:, tile_index, :]
+                right = words_of[group][:, which].rearrange("p c m -> p (c m)")[:, first : first + UNIT]
+                right_plane = proto_planes[4 * plane : P, column : column + UNIT]
             nc.tensor.matmul_mx(
-                out=acc,
-                lhsT=xv_codes[:, g, :].bitcast(FP8X4),
-                lhsT_scale=xv_planes[:, g, :],
-                rhs=codes_of[group][:, g, here].bitcast(FP8X4),
-                rhs_scale=planes_of[group][:, g, here],
-                start=start,
-                stop=stop,
+                out=accumulator(unit),
+                lhsT=left.bitcast(FP8X4),
+                lhsT_scale=left_plane,
+                rhs=right.bitcast(FP8X4),
+                rhs_scale=right_plane,
+                start=(number == order_of(unit)[0]),
+                stop=(number == order_of(unit)[-1]),
             )
 
-        def dot_pass(acc, group, g, here, start, stop):
-            nc.tensor.matmul_mx(
-                out=acc,
-                lhsT=x_codes[:, g, :].bitcast(FP8X4),
-                lhsT_scale=x_planes[:, g, :],
-                rhs=words_of[group][:, g, here].bitcast(FP8X4),
-                rhs_scale=proto_planes[
-                    4 * g : P, group * GROUP + here.start : group * GROUP + here.stop
-                ],
-                start=start,
-                stop=stop,
-            )
-
-        def multiply(group, numbers):
-            for number in numbers:
-                if number == 0:
-                    acc_of[group] = acc_pool.tile([P, GROUP], F32, name="acc")
-                one_pass = cross_pass if number < PASSES else dot_pass
-                one_pass(
-                    acc_of[group][:],
-                    group,
-                    number % PASSES,
-                    slice(0, GROUP),
-                    start=(number == 0),
-                    stop=(number == 2 * PASSES - 1),
-                )
-
-        def finish(group):
-            result = work.tile([P, GROUP], F32, name="result", bufs=6)
+        def finish(acc, shift, first, width):
+            result = work.tile([P, GROUP], F32, name="result", bufs=4)
             nc.vector.scalar_tensor_tensor(
-                out=result[:],
-                in0=acc_of[group][:],
+                out=result[:, :width],
+                in0=acc,
                 scalar=2.0,
-                in1=shift_of[group][:],
+                in1=shift,
                 op0=ALU.mult,
                 op1=ALU.subtract,
             )
-            nc.sync.dma_start(out=out_cols[:, group * GROUP : (group + 1) * GROUP], in_=result[:])
+            nc.sync.dma_start(out=out_cols[:, first : first + width], in_=result[:, :width])
 
-        def quantise_part(group, g, pair):
-            cols = slice(pair * PAIR, (pair + 1) * PAIR)
-            quantise(
-                grouped_of[group][:, g, cols, :].rearrange("p c t -> p (c t)"),
-                codes_of[group][:, g, cols],
-                planes_of[group][:, g, cols],
-            )
+        def finish_group(group):
+            finish(acc_of[group][:], shift_of[group][:], group * GROUP, GROUP)
 
-        def finish_pair(group, pair):
-            result = work.tile([P, GROUP], F32, name="result", bufs=6)
-            first = group * GROUP + pair * PAIR
-            nc.vector.scalar_tensor_tensor(
-                out=result[:, :PAIR],
-                in0=acc_of[(group, pair)][:, :PAIR],
-                scalar=2.0,
-                in1=shift_of[group][:, pair * PAIR : (pair + 1) * PAIR],
-                op0=ALU.mult,
-                op1=ALU.subtract,
-            )
-            nc.sync.dma_start(out=out_cols[:, first : first + PAIR], in_=result[:, :PAIR])
+        def finish_unit(unit):
+            half = unit % 2
+            shift = shift_of[unit // 2][:, half * UNIT : (half + 1) * UNIT]
+            finish(acc_of[unit][:, :UNIT], shift, unit * UNIT, UNIT)
 
-        tiles = [(group, t) for group in range(N_GROUPS) for t in range(GROUP // P)]
-        summed = 0
+        last = N_UNITS - 1
+        products = [(unit, number) for unit in range(last - 1) for number in order_of(unit)]
+        products += [(last - 1, number) for number in range(4)]
+        products = products[: -LEFT]
+        half_slots = 2 * N_UNITS - FIRST
+        products_at = {}
+        for half_slot in range(FIRST, 2 * N_UNITS):
+            begin = len(products) * (half_slot - FIRST) // half_slots
+            end = len(products) * (half_slot + 1 - FIRST) // half_slots
+            products_at[half_slot] = products[begin:end]
 
-        def sum_next(count):
-            for group, t in tiles[summed : summed + count]:
-                if group not in sums_of:
-                    sums_of[group] = work.tile([P, GROUP // P], F32, name="sums", bufs=3)
-                sum_rows(group, t)
-            return summed + count
+        def half_slot_of(product):
+            return ([h for h in products_at if product in products_at[h]] + [2 * N_UNITS])[0]
 
-        def new_codes(group):
-            codes_of[group] = codes_pool.tile([P, PASSES, GROUP], U32, name="codes", align_bytes=64)
-            planes_of[group] = codes_pool.tile([P, PASSES, GROUP], U8, name="planes", align_bytes=64)
+        sorts_at = {half_slot_of((2 * group, 4)) - 1: group for group in range(N_GROUPS - 1)}
+        finishes_at = {half_slot_of((2 * group + 1, 9)) // 2 + 1: group for group in range(N_GROUPS - 1)}
+        loads_at = {
+            2: [(load_words, 0), (load_words, 1), (load_rows, 7), (load_rows, 8), (load_words, 2), (load_rows, 9)],
+            3: [(load_rows, 10)],
+        }
+        for group in range(3, N_GROUPS):
+            slot = half_slot_of((2 * group - 5, 9)) // 2
+            loads_at.setdefault(slot, []).append((load_words, group))
+            for unit in (2 * group + 5, 2 * group + 6):
+                if unit < N_UNITS:
+                    loads_at[slot].append((load_rows, unit))
 
-        for step in range(N_GROUPS):
-            rooted, quantised, multiplied = step, step - 1, step - 3
-            last = step == N_GROUPS - 1
-            sums_left = SUMS_IN_STEP[step]
-            grouped_of[rooted] = grouped_pool.tile(
-                [P, PASSES, GROUP, PACK], BF16, name="grouped", align_bytes=64
-            )
-            if live(quantised):
-                new_codes(quantised)
-                for half in range(2):
-                    quantise_half(quantised, half)
-                    if sums_left:
-                        summed = sum_next(1)
-                        sums_left -= 1
-            for quarter in range(4):
-                for g in (2 * (quarter % 2), 2 * (quarter % 2) + 1):
-                    transpose_and_root(rooted, quarter // 2, g)
-                if live(quantised) and quarter >= 2:
-                    spread_sums(quantised, 2 * quarter - 4)
-                    spread_sums(quantised, 2 * quarter - 3)
-                if live(multiplied):
-                    multiply(multiplied, (2 * quarter, 2 * quarter + 1))
-                if last:
-                    multiply(rooted - 2 + quarter // 2, (2 * (quarter % 2), 2 * (quarter % 2) + 1))
-            if step == 0:
-                transpose_xv_and_root()
-                summed = sum_next(4)
-                sums_left -= 4
-                sum_xv()
+        for slot in range(N_UNITS):
+            tiles = list(range(2 * slot + (slot > 7), 2 * slot + 2 + (slot >= 7)))
+            tiles = [t for t in tiles if t < 2 * N_UNITS]
+            sum_tile(tiles[0])
+            if slot == 0:
+                sort_x()
+            if slot >= 1:
+                quantise_unit(slot - 1)
+            if slot == 2:
                 make_pixel_term()
-            if step == 1:
-                transpose_x_and_copy()
-            summed = sum_next(sums_left)
-            if live(quantised):
-                make_shift(quantised)
-            if step == 1:
                 quantise_xv()
+            for half in range(2):
+                for g in (2 * half, 2 * half + 1):
+                    transpose_and_root(slot, g)
+                if 2 <= 2 * slot + half < 5:
+                    transpose_x(2 * slot + half - 2)
+                    copy_x(2 * slot + half - 2)
+                if half == 1 and slot >= 2 and slot % 2 == 0:
+                    spread_sums(slot // 2 - 1)
+                if 2 * slot + half in sorts_at:
+                    sort_words(sorts_at[2 * slot + half])
+                for unit, number in products_at.get(2 * slot + half, []):
+                    multiply(unit, number)
+            if slot == 1:
+                transpose_xv_and_root()
+            for tile_index in tiles[1:]:
+                sum_tile(tile_index)
+            if slot == 2:
                 quantise_x()
-            if live(multiplied):
-                finish(multiplied)
-            if live(step + ROW_GROUPS):
-                load_rows(step + ROW_GROUPS)
-            if live(step + 2):
-                load_words(step + 2)
+                zero_other_halves()
+            if slot >= 3 and slot % 2 == 1:
+                make_shift(slot // 2 - 1)
+            if slot in finishes_at:
+                finish_group(finishes_at[slot])
+            for load, number in loads_at.get(slot, []):
+                load(number)
 
-        final = N_GROUPS - 1
-        halves = [slice(pair * PAIR, (pair + 1) * PAIR) for pair in range(PAIRS)]
-        new_codes(final)
-        for g in range(PASSES):
-            quantise_part(final, g, 0)
-        for group in (final - 2, final - 1):
-            multiply(group, range(PASSES, 2 * PASSES))
-            finish(group)
-        for t in range(GROUP // P):
-            spread_sums(final, t)
-        make_shift(final)
-        for pair in range(PAIRS):
-            acc_of[(final, pair)] = acc_pool.tile([P, GROUP], F32, name="acc")
-        for g in range(PASSES):
-            for pair, here in enumerate(halves):
-                dot_pass(acc_of[(final, pair)][:, :PAIR], final, g, here, start=(g == 0), stop=False)
-        for pair, here in enumerate(halves):
-            for g in range(PASSES):
-                if pair == 1:
-                    quantise_part(final, g, 1)
-                cross_pass(
-                    acc_of[(final, pair)][:, :PAIR],
-                    final,
-                    g,
-                    here,
-                    start=False,
-                    stop=(g == PASSES - 1),
-                )
-        for pair in range(PAIRS):
-            finish_pair(final, pair)
+        spread_sums(N_GROUPS - 1)
+        make_shift(N_GROUPS - 1)
+        quantise_part(last, 0)
+        sort_words(N_GROUPS - 1)
+        finish_group(N_GROUPS - 2)
+        for g in range(1, PASSES):
+            quantise_part(last, g)
+        done = set(products)
+        for unit in (last - 2, last - 1):
+            for number in order_of(unit)[: 8 if unit == last - 1 else 10]:
+                if (unit, number) not in done:
+                    multiply(unit, number)
+        for number in order_of(last)[:7]:
+            multiply(last, number)
+        for number in (8, 9):
+            multiply(last - 1, number)
+        finish_unit(last - 1)
+        for number in order_of(last)[7:]:
+            multiply(last, number)
+        finish_unit(last)

@@ -30,6 +30,7 @@ UNIT_PASSES = 10
 FIRST = 13
 LEFT = 4
 LAM = 1.0 / D
+FOLDED = range(2, 8)
 
 FLOPS = 2 * 2 * P * N_PROTO * D
 
@@ -116,6 +117,10 @@ def tile_probprotoseghead_w_e_kernel(
         nc.gpsimd.memset(zeros[:].bitcast(I32), 0)
         ident = const.tile([P, P], F32, name="ident")
         make_identity(nc, ident[:])
+        ident_bf16 = const.tile([P, P], BF16, name="ident_bf16")
+        make_identity(nc, ident_bf16[:])
+        ones = const.tile([P, P], F32, name="ones")
+        nc.gpsimd.memset(ones[:], 1.0)
 
         load_first_rows()
         load_rows(1)
@@ -241,6 +246,7 @@ def tile_probprotoseghead_w_e_kernel(
 
         grouped_of = {}
         sums_of = {}
+        folded_of = {}
         codes_of = {}
         planes_of = {}
         spread_of = {}
@@ -307,9 +313,33 @@ def tile_probprotoseghead_w_e_kernel(
                 in_=raw_of[group][:].bitcast(I32).rearrange("p c (j m) -> p j c m", j=2),
             )
 
+        def fold_tile(group):
+            unit = 2 * group + 1
+            bank = banks.tile([P, GROUP], F32, name="bank")
+            for c in range(D // P):
+                g, k = c // 4, c % 4 * P
+                nc.tensor.matmul(
+                    bank[:, :P],
+                    lhsT=rows_of[unit][:, g, 1, k : k + P],
+                    rhs=ident_bf16[:],
+                    start=(c == 0),
+                    stop=(c == D // P - 1),
+                )
+            folded_of[group] = work.tile([P, P], F32, name="folded")
+            nc.vector.tensor_copy(out=folded_of[group][:], in_=bank[:, :P])
+
         def spread_sums(group):
             spread_of[group] = spread_pool.tile([P, GROUP], F32, name="spread")
             for column in range(4):
+                if column == 3 and group in FOLDED:
+                    nc.tensor.matmul(
+                        spread_of[group][:, column * P : (column + 1) * P],
+                        lhsT=ones[:],
+                        rhs=folded_of[group][:],
+                        start=True,
+                        stop=True,
+                    )
+                    continue
                 nc.tensor.transpose(
                     spread_of[group][:, column * P : (column + 1) * P],
                     sums_of[group][:, column : column + 1].to_broadcast([P, P]),
@@ -414,8 +444,7 @@ def tile_probprotoseghead_w_e_kernel(
                     loads_at[slot].append((load_rows, unit))
 
         for slot in range(N_UNITS):
-            tiles = list(range(2 * slot + (slot > 7), 2 * slot + 2 + (slot >= 7)))
-            tiles = [t for t in tiles if t < 2 * N_UNITS]
+            tiles = [t for t in (2 * slot, 2 * slot + 1) if not (t % 4 == 3 and t // 4 in FOLDED)]
             sum_tile(tiles[0])
             if slot == 0:
                 sort_x()
@@ -436,6 +465,8 @@ def tile_probprotoseghead_w_e_kernel(
                     sort_words(sorts_at[2 * slot + half])
                 for unit, number in products_at.get(2 * slot + half, []):
                     multiply(unit, number)
+                if half == 0 and slot % 2 == 1 and slot // 2 in FOLDED:
+                    fold_tile(slot // 2)
             if slot == 1:
                 transpose_xv_and_root()
             for tile_index in tiles[1:]:

@@ -313,23 +313,29 @@ def tile_probprotoseghead_w_e_kernel(
                 in_=raw_of[group][:].bitcast(I32).rearrange("p c (j m) -> p j c m", j=2),
             )
 
+        def new_spread(group):
+            spread_of[group] = spread_pool.tile([P, GROUP], F32, name="spread")
+
         def fold_tile(group):
             unit = 2 * group + 1
-            bank = banks.tile([P, GROUP], F32, name="bank")
+            new_spread(group)
             for c in range(D // P):
                 g, k = c // 4, c % 4 * P
                 nc.tensor.matmul(
-                    bank[:, :P],
+                    spread_of[group][:, 3 * P :],
                     lhsT=rows_of[unit][:, g, 1, k : k + P],
                     rhs=ident_bf16[:],
                     start=(c == 0),
                     stop=(c == D // P - 1),
                 )
+
+        def keep_folded(group):
             folded_of[group] = work.tile([P, P], F32, name="folded")
-            nc.vector.tensor_copy(out=folded_of[group][:], in_=bank[:, :P])
+            nc.vector.tensor_copy(out=folded_of[group][:], in_=spread_of[group][:, 3 * P :])
 
         def spread_sums(group):
-            spread_of[group] = spread_pool.tile([P, GROUP], F32, name="spread")
+            if group not in FOLDED:
+                new_spread(group)
             for column in range(4):
                 if column == 3 and group in FOLDED:
                     nc.tensor.matmul(
@@ -433,34 +439,47 @@ def tile_probprotoseghead_w_e_kernel(
         sorts_at = {half_slot_of((2 * group, 4)) - 1: group for group in range(N_GROUPS - 1)}
         finishes_at = {half_slot_of((2 * group + 1, 9)) // 2 + 1: group for group in range(N_GROUPS - 1)}
         loads_at = {
-            2: [(load_words, 0), (load_words, 1), (load_rows, 7), (load_rows, 8), (load_words, 2), (load_rows, 9)],
-            3: [(load_rows, 10)],
+            2: [(load_words, 0), (load_words, 1), (load_rows, 7), (load_words, 2), (load_rows, 8)],
+            3: [(load_rows, 9)],
         }
         for group in range(3, N_GROUPS):
             slot = half_slot_of((2 * group - 5, 9)) // 2
             loads_at.setdefault(slot, []).append((load_words, group))
-            for unit in (2 * group + 5, 2 * group + 6):
-                if unit < N_UNITS:
-                    loads_at[slot].append((load_rows, unit))
+            for unit in range(2 * group + 4, min(2 * group + 6, N_UNITS)):
+                loads_at[slot].append((load_rows, unit))
+
+        on_vector = [t for t in range(2 * N_UNITS) if not (t % 4 == 3 and t // 4 in FOLDED)]
+        even_from = 2 * FOLDED[0]
+        later = on_vector[2 * even_from :]
+
+        def tiles_of(slot):
+            if slot < even_from:
+                return on_vector[2 * slot : 2 * slot + 2]
+            ends = [len(later) * (s - even_from) // (last - even_from) for s in (slot, slot + 1)]
+            return later[ends[0] : ends[1]]
 
         for slot in range(N_UNITS):
-            tiles = [t for t in (2 * slot, 2 * slot + 1) if not (t % 4 == 3 and t // 4 in FOLDED)]
-            sum_tile(tiles[0])
-            if slot == 0:
-                sort_x()
+            tiles = tiles_of(slot)
+            for tile_index in tiles[:1]:
+                sum_tile(tile_index)
             if slot >= 1:
                 quantise_unit(slot - 1)
+            if slot == 1:
+                sort_x()
             if slot == 2:
                 make_pixel_term()
                 quantise_xv()
             for half in range(2):
                 for g in (2 * half, 2 * half + 1):
                     transpose_and_root(slot, g)
-                if 2 <= 2 * slot + half < 5:
-                    transpose_x(2 * slot + half - 2)
-                    copy_x(2 * slot + half - 2)
+                if 3 <= 2 * slot + half < 6:
+                    transpose_x(2 * slot + half - 3)
+                    copy_x(2 * slot + half - 3)
                 if half == 1 and slot >= 2 and slot % 2 == 0:
                     spread_sums(slot // 2 - 1)
+                if half == 1 and slot == last:
+                    keep_folded(N_GROUPS - 1)
+                    spread_sums(N_GROUPS - 1)
                 if 2 * slot + half in sorts_at:
                     sort_words(sorts_at[2 * slot + half])
                 for unit, number in products_at.get(2 * slot + half, []):
@@ -471,29 +490,34 @@ def tile_probprotoseghead_w_e_kernel(
                 transpose_xv_and_root()
             for tile_index in tiles[1:]:
                 sum_tile(tile_index)
+            if slot % 2 == 1 and slot // 2 in FOLDED and slot < last:
+                keep_folded(slot // 2)
             if slot == 2:
                 quantise_x()
                 zero_other_halves()
-            if slot >= 3 and slot % 2 == 1:
+            if slot >= 2 and slot % 2 == 0:
                 make_shift(slot // 2 - 1)
             if slot in finishes_at:
                 finish_group(finishes_at[slot])
+            if slot == last:
+                sort_words(N_GROUPS - 1)
+                make_shift(N_GROUPS - 1)
+                quantise_part(last, 0)
+                quantise_part(last, 1)
             for load, number in loads_at.get(slot, []):
                 load(number)
 
-        spread_sums(N_GROUPS - 1)
-        make_shift(N_GROUPS - 1)
-        quantise_part(last, 0)
-        sort_words(N_GROUPS - 1)
-        finish_group(N_GROUPS - 2)
-        for g in range(1, PASSES):
-            quantise_part(last, g)
         done = set(products)
         for unit in (last - 2, last - 1):
             for number in order_of(unit)[: 8 if unit == last - 1 else 10]:
                 if (unit, number) not in done:
                     multiply(unit, number)
-        for number in order_of(last)[:7]:
+        for number in order_of(last)[:4]:
+            multiply(last, number)
+        quantise_part(last, 2)
+        finish_group(N_GROUPS - 2)
+        quantise_part(last, 3)
+        for number in order_of(last)[4:7]:
             multiply(last, number)
         for number in (8, 9):
             multiply(last - 1, number)

@@ -123,25 +123,35 @@ def tile_probprotoseghead_w_e_kernel(
         nc.gpsimd.memset(ones[:], 1.0)
 
         load_first_rows()
-        load_rows(1)
         x_rows = const.tile([P, D], BF16, name="x_rows")
-        nc.sync.dma_start(out=x_rows[:], in_=x)
-        staged_scales = const.tile([BLOCKS, N_PROTO], U8, name="staged_scales", align_bytes=64)
-        nc.sync.dma_start(
-            out=staged_scales[:].bitcast(I32).rearrange("b (c w) -> b c w", c=CLASSES),
-            in_=scale_view.bitcast(I32),
-        )
         xv_rows = const.tile([P, D], BF16, name="xv_rows")
-        nc.sync.dma_start(out=xv_rows[:], in_=x_var)
-        load_rows(2)
-        for plane in range(4):
+        staged_scales = const.tile([BLOCKS, N_PROTO], U8, name="staged_scales", align_bytes=64)
+
+        def place_scales(plane):
             for r in range(4):
                 rows = slice(2 * r + plane, 32, 8) if plane < 2 else slice(16 * plane + r, 16 * plane + 16, 4)
                 nc.sync.dma_start(
                     out=proto_planes[4 * plane + r : P : 32, :].bitcast(I32),
                     in_=staged_scales[rows, :].bitcast(I32),
                 )
-            load_rows(3 + plane)
+
+        load_rows(1)
+        nc.sync.dma_start(out=x_rows[:], in_=x)
+        load_rows(2)
+        nc.sync.dma_start(out=xv_rows[:], in_=x_var)
+        nc.sync.dma_start(
+            out=staged_scales[:].bitcast(I32).rearrange("b (c w) -> b c w", c=CLASSES),
+            in_=scale_view.bitcast(I32),
+        )
+        load_rows(3)
+        load_rows(4)
+        load_rows(5)
+        place_scales(0)
+        place_scales(1)
+        place_scales(2)
+        place_scales(3)
+        load_words(0)
+        load_rows(6)
 
         xs = const.tile([P, 2, 2, 2, P], F32, name="xs")
         xv_grouped = const.tile([P, PASSES, P, PACK], BF16, name="xv_grouped", align_bytes=64)
@@ -439,7 +449,7 @@ def tile_probprotoseghead_w_e_kernel(
         sorts_at = {half_slot_of((2 * group, 4)) - 1: group for group in range(N_GROUPS - 1)}
         finishes_at = {half_slot_of((2 * group + 1, 9)) // 2 + 1: group for group in range(N_GROUPS - 1)}
         loads_at = {
-            2: [(load_words, 0), (load_words, 1), (load_rows, 7), (load_words, 2), (load_rows, 8)],
+            2: [(load_words, 1), (load_rows, 7), (load_words, 2), (load_rows, 8)],
             3: [(load_rows, 9)],
         }
         for group in range(3, N_GROUPS):

@@ -150,8 +150,6 @@ def tile_probprotoseghead_w_e_kernel(
         place_scales(1)
         place_scales(2)
         place_scales(3)
-        load_words(0)
-        load_rows(6)
 
         xs = const.tile([P, 2, 2, 2, P], F32, name="xs")
         xv_grouped = const.tile([P, PASSES, P, PACK], BF16, name="xv_grouped", align_bytes=64)
@@ -449,7 +447,7 @@ def tile_probprotoseghead_w_e_kernel(
         sorts_at = {half_slot_of((2 * group, 4)) - 1: group for group in range(N_GROUPS - 1)}
         finishes_at = {half_slot_of((2 * group + 1, 9)) // 2 + 1: group for group in range(N_GROUPS - 1)}
         loads_at = {
-            2: [(load_words, 1), (load_rows, 7), (load_words, 2), (load_rows, 8)],
+            2: [(load_words, 0), (load_rows, 6), (load_words, 1), (load_rows, 7), (load_words, 2), (load_rows, 8)],
             3: [(load_rows, 9)],
         }
         for group in range(3, N_GROUPS):

@@ -111,12 +111,14 @@ def tile_probprotoseghead_w_e_kernel(
                 )
             words_of[group] = words
 
-        proto_planes = const.tile([P, N_PROTO], U8, name="proto_planes", align_bytes=64)
-        nc.vector.memset(proto_planes[:].bitcast(I32), 0)
+        run_planes = const.tile([P, N_PROTO], U8, name="run_planes", align_bytes=64)
+        plain_planes = const.tile([P, N_PROTO], U8, name="plain_planes", align_bytes=64)
+        staged_scales = const.tile([P, N_PROTO], U8, name="staged_scales", align_bytes=64)
         zeros = const.tile([P, 2, P], U32, name="zeros")
         nc.gpsimd.memset(zeros[:].bitcast(I32), 0)
         ident = const.tile([P, P], F32, name="ident")
         make_identity(nc, ident[:])
+        nc.gpsimd.memset(staged_scales[:].bitcast(I32), 0)
         ident_bf16 = const.tile([P, P], BF16, name="ident_bf16")
         make_identity(nc, ident_bf16[:])
         ones = const.tile([P, P], F32, name="ones")
@@ -125,31 +127,32 @@ def tile_probprotoseghead_w_e_kernel(
         load_first_rows()
         x_rows = const.tile([P, D], BF16, name="x_rows")
         xv_rows = const.tile([P, D], BF16, name="xv_rows")
-        staged_scales = const.tile([BLOCKS, N_PROTO], U8, name="staged_scales", align_bytes=64)
 
-        def place_scales(plane):
+        def place_scales(planes, first):
             for r in range(4):
-                rows = slice(2 * r + plane, 32, 8) if plane < 2 else slice(16 * plane + r, 16 * plane + 16, 4)
+                begin = first + 2 * r
                 nc.sync.dma_start(
-                    out=proto_planes[4 * plane + r : P : 32, :].bitcast(I32),
-                    in_=staged_scales[rows, :].bitcast(I32),
+                    out=planes[r:P:4, :].bitcast(I32), in_=staged_scales[begin : begin + 32, :].bitcast(I32)
                 )
 
         load_rows(1)
         nc.sync.dma_start(out=x_rows[:], in_=x)
         load_rows(2)
         nc.sync.dma_start(out=xv_rows[:], in_=x_var)
-        nc.sync.dma_start(
-            out=staged_scales[:].bitcast(I32).rearrange("b (c w) -> b c w", c=CLASSES),
-            in_=scale_view.bitcast(I32),
-        )
+        for rows, blocks in (
+            (slice(0, 32), slice(0, 32)),
+            (slice(32, 64, 2), slice(32, 48)),
+            (slice(33, 64, 2), slice(48, 64)),
+        ):
+            nc.sync.dma_start(
+                out=staged_scales[rows, :].bitcast(I32).rearrange("b (c w) -> b c w", c=CLASSES),
+                in_=scale_view[blocks].bitcast(I32),
+            )
         load_rows(3)
         load_rows(4)
         load_rows(5)
-        place_scales(0)
-        place_scales(1)
-        place_scales(2)
-        place_scales(3)
+        place_scales(run_planes, 0)
+        place_scales(plain_planes, 32)
 
         xs = const.tile([P, 2, 2, 2, P], F32, name="xs")
         xv_grouped = const.tile([P, PASSES, P, PACK], BF16, name="xv_grouped", align_bytes=64)
@@ -394,12 +397,12 @@ def tile_probprotoseghead_w_e_kernel(
             else:
                 if number < 8:
                     j, ab = number // 2 % 2, number % 2
-                    tile_index, which, plane = 2 * ab + (ab + j) % 2, j, ab
+                    tile_index, which, plane, scales = 2 * ab + (ab + j) % 2, j, ab, run_planes
                 else:
-                    tile_index, which, plane = number - 4, number - 6, number - 6
+                    tile_index, which, plane, scales = number - 4, number - 6, number - 8, plain_planes
                 left, left_plane = x_codes[:, tile_index, :], x_planes[:, tile_index, :]
                 right = words_of[group][:, which].rearrange("p c m -> p (c m)")[:, first : first + UNIT]
-                right_plane = proto_planes[4 * plane : P, column : column + UNIT]
+                right_plane = scales[4 * plane : P, column : column + UNIT]
             nc.tensor.matmul_mx(
                 out=accumulator(unit),
                 lhsT=left.bitcast(FP8X4),

@@ -102,7 +102,11 @@ def tile_probprotoseghead_w_e_kernel(
         def load_words(group):
             classes = slice(group * GROUP_CLASSES, (group + 1) * GROUP_CLASSES)
             raw = raw_pool.tile([P, GROUP_CLASSES, 2 * PER_CLASS], U32, name="raw", align_bytes=64)
-            nc.sync.dma_start(out=raw[:].bitcast(I32), in_=run_view[:, classes, :].bitcast(I32))
+            for h in range(2):
+                nc.sync.dma_start(
+                    out=raw[h:P:2].bitcast(I32),
+                    in_=run_view[h * P // 2 : (h + 1) * P // 2, classes, :].bitcast(I32),
+                )
             raw_of[group] = raw
             words = words_pool.tile([P, 4, GROUP_CLASSES, PER_CLASS], U32, name="words", align_bytes=64)
             for g in (2, 3):
@@ -139,14 +143,13 @@ def tile_probprotoseghead_w_e_kernel(
         nc.sync.dma_start(out=x_rows[:], in_=x)
         load_rows(2)
         nc.sync.dma_start(out=xv_rows[:], in_=x_var)
-        for rows, blocks in (
-            (slice(0, 32), slice(0, 32)),
-            (slice(32, 64, 2), slice(32, 48)),
-            (slice(33, 64, 2), slice(48, 64)),
-        ):
+        for g in range(PASSES):
+            begin = 32 * (g // 2) + g % 2
             nc.sync.dma_start(
-                out=staged_scales[rows, :].bitcast(I32).rearrange("b (c w) -> b c w", c=CLASSES),
-                in_=scale_view[blocks].bitcast(I32),
+                out=staged_scales[begin : begin + 32 : 2, :]
+                .bitcast(I32)
+                .rearrange("b (c w) -> b c w", c=CLASSES),
+                in_=scale_view[16 * g : 16 * g + 16].bitcast(I32),
             )
         load_rows(3)
         load_rows(4)
@@ -154,7 +157,7 @@ def tile_probprotoseghead_w_e_kernel(
         place_scales(run_planes, 0)
         place_scales(plain_planes, 32)
 
-        xs = const.tile([P, 2, 2, 2, P], F32, name="xs")
+        swapped = const.tile([P, 2, 2, P], F32, name="swapped")
         xv_grouped = const.tile([P, PASSES, P, PACK], BF16, name="xv_grouped", align_bytes=64)
         x_grouped = const.tile([P, 6, P, PACK], BF16, name="x_grouped", align_bytes=64)
         xv_codes = const.tile([P, PASSES, P], U32, name="xv_codes", align_bytes=64)
@@ -165,24 +168,25 @@ def tile_probprotoseghead_w_e_kernel(
         pixel_term = const.tile([P, 1], F32, name="pixel_term")
 
         def sort_x():
-            source = x_rows[:, : D // 2].bitcast(F32).rearrange("p (c v i j u) -> p v j u c i", c=16, v=2, i=4, j=2)
-            dest = xs[:].rearrange("p v s u (c j i) -> p v s j u c i", j=2, i=4)
-            for ab in range(2):
-                for sw in range(2):
-                    for jj in range(2):
-                        nc.vector.tensor_copy(out=dest[:, ab, sw, jj], in_=source[:, ab, (jj + sw) % 2])
+            source = x_rows[:, : D // 2].bitcast(F32).rearrange("p (g s h u) -> p h g u s", g=2, h=2, u=2)
+            dest = swapped[:].rearrange("p g u (s h) -> p h g u s", h=2)
+            for h in range(2):
+                nc.vector.tensor_copy(out=dest[:, h], in_=source[:, 1 - h])
 
         x_banks = {}
 
         def transpose_x(b):
             bank = banks.tile([P, GROUP], F32, name="bank")
             x_words = x_rows[:].bitcast(F32)
+            pass_of = {0: 0, 2: 1, 4: 2, 5: 3}
             transpose_four(
                 bank,
                 [
-                    xs[:, b, v, u, :] if b < 2 else x_words[:, 2 * P * (2 + v) + u : 2 * P * (3 + v) : 2]
+                    swapped[:, tile_index // 2, u, :]
+                    if tile_index in (1, 3)
+                    else x_words[:, 2 * P * pass_of[tile_index] + u : 2 * P * (pass_of[tile_index] + 1) : 2]
                     for u in range(2)
-                    for v in range(2)
+                    for tile_index in (2 * b, 2 * b + 1)
                 ],
             )
             x_banks[b] = bank
@@ -205,12 +209,10 @@ def tile_probprotoseghead_w_e_kernel(
 
         def zero_other_halves():
             for ab in range(2):
-                for i in range(4):
-                    start = 4 * (1 - ab) + i
-                    nc.sync.dma_start(
-                        out=x_codes[start : P : 8, 2 * ab : 2 * ab + 2, :].bitcast(I32),
-                        in_=zeros[start : P : 8, :, :].bitcast(I32),
-                    )
+                nc.sync.dma_start(
+                    out=x_codes[1 - ab : P : 2, 2 * ab : 2 * ab + 2, :].bitcast(I32),
+                    in_=zeros[1 - ab : P : 2, :, :].bitcast(I32),
+                )
 
         def transpose_xv_and_root():
             xv_words = xv_rows[:].bitcast(F32)

@@ -10,6 +10,7 @@ U8 = mybir.dt.uint8
 I32 = mybir.dt.int32
 FP8X4 = mybir.dt.float8_e4m3fn_x4
 ALU = mybir.AluOpType
+AXIS_X = mybir.AxisListType.X
 SQRT = mybir.ActivationFunctionType.Sqrt
 
 P = 128
@@ -27,7 +28,7 @@ GROUP = 512
 N_GROUPS = N_PROTO // GROUP
 GROUP_CLASSES = GROUP // PER_CLASS
 UNIT_PASSES = 10
-FIRST = 13
+FIRST = 12
 LEFT = 4
 LAM = 1.0 / D
 FOLDED = range(2, 8)
@@ -125,8 +126,6 @@ def tile_probprotoseghead_w_e_kernel(
         nc.gpsimd.memset(staged_scales[:].bitcast(I32), 0)
         ident_bf16 = const.tile([P, P], BF16, name="ident_bf16")
         make_identity(nc, ident_bf16[:])
-        ones = const.tile([P, P], F32, name="ones")
-        nc.gpsimd.memset(ones[:], 1.0)
 
         load_first_rows()
         x_rows = const.tile([P, D], BF16, name="x_rows")
@@ -259,7 +258,6 @@ def tile_probprotoseghead_w_e_kernel(
 
         grouped_of = {}
         sums_of = {}
-        folded_of = {}
         codes_of = {}
         planes_of = {}
         spread_of = {}
@@ -336,29 +334,21 @@ def tile_probprotoseghead_w_e_kernel(
                 g, k = c // 4, c % 4 * P
                 nc.tensor.matmul(
                     spread_of[group][:, 3 * P :],
-                    lhsT=rows_of[unit][:, g, 1, k : k + P],
-                    rhs=ident_bf16[:],
+                    lhsT=ident_bf16[:],
+                    rhs=rows_of[unit][:, g, 1, k : k + P],
                     start=(c == 0),
                     stop=(c == D // P - 1),
                 )
 
-        def keep_folded(group):
-            folded_of[group] = work.tile([P, P], F32, name="folded")
-            nc.vector.tensor_copy(out=folded_of[group][:], in_=spread_of[group][:, 3 * P :])
+        def sum_folded(group):
+            nc.vector.tensor_reduce(
+                out=sums_of[group][:, 3:4], in_=spread_of[group][:, 3 * P :], op=ALU.add, axis=AXIS_X
+            )
 
         def spread_sums(group):
             if group not in FOLDED:
                 new_spread(group)
             for column in range(4):
-                if column == 3 and group in FOLDED:
-                    nc.tensor.matmul(
-                        spread_of[group][:, column * P : (column + 1) * P],
-                        lhsT=ones[:],
-                        rhs=folded_of[group][:],
-                        start=True,
-                        stop=True,
-                    )
-                    continue
                 nc.tensor.transpose(
                     spread_of[group][:, column * P : (column + 1) * P],
                     sums_of[group][:, column : column + 1].to_broadcast([P, P]),
@@ -491,7 +481,7 @@ def tile_probprotoseghead_w_e_kernel(
                 if half == 1 and slot >= 2 and slot % 2 == 0:
                     spread_sums(slot // 2 - 1)
                 if half == 1 and slot == last:
-                    keep_folded(N_GROUPS - 1)
+                    sum_folded(N_GROUPS - 1)
                     spread_sums(N_GROUPS - 1)
                 if 2 * slot + half in sorts_at:
                     sort_words(sorts_at[2 * slot + half])
@@ -504,7 +494,7 @@ def tile_probprotoseghead_w_e_kernel(
             for tile_index in tiles[1:]:
                 sum_tile(tile_index)
             if slot % 2 == 1 and slot // 2 in FOLDED and slot < last:
-                keep_folded(slot // 2)
+                sum_folded(slot // 2)
             if slot == 2:
                 quantise_x()
                 zero_other_halves()

from contextlib import ExitStack

import concourse.mybir as mybir
from concourse.masks import make_identity

F32 = mybir.dt.float32
BF16 = mybir.dt.bfloat16
U32 = mybir.dt.uint32
U8 = mybir.dt.uint8
I32 = mybir.dt.int32
FP8X4 = mybir.dt.float8_e4m3fn_x4
ALU = mybir.AluOpType
AXIS_X = mybir.AxisListType.X
SQRT = mybir.ActivationFunctionType.Sqrt

P = 128
D = 2048
PACK = 4
K_PASS = P * PACK
PASSES = D // K_PASS
BLOCKS = D // 32
CLASSES = 64
PER_CLASS = 64
N_PROTO = CLASSES * PER_CLASS
UNIT = 2 * P
N_UNITS = N_PROTO // UNIT
GROUP = 512
N_GROUPS = N_PROTO // GROUP
GROUP_CLASSES = GROUP // PER_CLASS
UNIT_PASSES = 10
FIRST = 12
LEFT = 4
LAM = 1.0 / D
FOLDED = range(2, 8)

FLOPS = 2 * 2 * P * N_PROTO * D


def tile_probprotoseghead_w_e_kernel(
    tc, x, x_var, prototypes_words, prototypes_scales, proto_var, out
):
    nc = tc.nc
    var_rows = proto_var.rearrange("c m d -> (c m) d")
    run_view = prototypes_words.rearrange("(c g) p m t -> c (g p m t)", g=PASSES).rearrange(
        "c (a q b) -> a q c b", a=2, q=P
    )[0]
    word_view = prototypes_words.rearrange("(c g) p m t -> g p c (m t)", g=PASSES)
    scale_view = prototypes_scales.rearrange("(c g) q m -> (g q) c m", g=PASSES)
    out_cols = out.rearrange("n c m -> n (c m)")

    with ExitStack() as stack:
        const = stack.enter_context(tc.tile_pool(name="const", bufs=1))
        rows_pool = stack.enter_context(tc.tile_pool(name="rows", bufs=7))
        raw_pool = stack.enter_context(tc.tile_pool(name="raw", bufs=3))
        words_pool = stack.enter_context(tc.tile_pool(name="words", bufs=3))
        grouped_pool = stack.enter_context(tc.tile_pool(name="grouped", bufs=2))
        codes_pool = stack.enter_context(tc.tile_pool(name="codes", bufs=6))
        work = stack.enter_context(tc.tile_pool(name="work", bufs=2))
        banks = stack.enter_context(tc.psum_pool(name="banks", bufs=4))
        acc_pool = stack.enter_context(tc.psum_pool(name="acc", bufs=3))
        spread_pool = stack.enter_context(tc.psum_pool(name="spread", bufs=1))
        stack.enter_context(tc.manual_schedule())

        def transpose_four(bank, blocks):
            for slot, block in enumerate(blocks):
                nc.tensor.transpose(bank[:, slot * P : (slot + 1) * P], block, ident[:])

        def quantise(grouped, codes, planes):
            nc.vector.quantize_mx(out=codes.bitcast(FP8X4), scales=planes, in_=grouped)

        def sum_row(first_half, second_half, total):
            junk = work.tile([P, 2, D // 4], F32, name="junk")
            nc.vector.scalar_tensor_tensor(
                out=junk[:],
                in0=first_half,
                scalar=1.0,
                in1=second_half,
                op0=ALU.mult,
                op1=ALU.add,
                accum_out=total,
            )

        rows_of = {}
        raw_of = {}
        words_of = {}

        def source_of(unit):
            return var_rows[unit * UNIT : (unit + 1) * UNIT, :].rearrange("(p t) d -> p t d", t=2)

        def load_first_rows():
            rows = const.tile([P, PASSES, 2, K_PASS], BF16, name="first_rows")
            for g in range(PASSES):
                nc.sync.dma_start(
                    out=rows[:, g, :, :], in_=source_of(0)[:, :, g * K_PASS : (g + 1) * K_PASS]
                )
            rows_of[0] = rows[:]

        def load_rows(unit):
            rows = rows_pool.tile([P, 2, D], BF16, name="rows")
            nc.sync.dma_start(out=rows[:], in_=source_of(unit))
            rows_of[unit] = rows[:].rearrange("p t (g k) -> p g t k", g=PASSES)

        def load_words(group):
            classes = slice(group * GROUP_CLASSES, (group + 1) * GROUP_CLASSES)
            raw = raw_pool.tile([P, GROUP_CLASSES, 2 * PER_CLASS], U32, name="raw", align_bytes=64)
            for h in range(2):
                nc.sync.dma_start(
                    out=raw[h:P:2].bitcast(I32),
                    in_=run_view[h * P // 2 : (h + 1) * P // 2, classes, :].bitcast(I32),
                )
            raw_of[group] = raw
            words = words_pool.tile([P, 4, GROUP_CLASSES, PER_CLASS], U32, name="words", align_bytes=64)
            for g in (2, 3):
                nc.sync.dma_start(
                    out=words[:, g].bitcast(I32), in_=word_view[g][:, classes, :].bitcast(I32)
                )
            words_of[group] = words

        run_planes = const.tile([P, N_PROTO], U8, name="run_planes", align_bytes=64)
        plain_planes = const.tile([P, N_PROTO], U8, name="plain_planes", align_bytes=64)
        staged_scales = const.tile([P, N_PROTO], U8, name="staged_scales", align_bytes=64)
        zeros = const.tile([P, 2, P], U32, name="zeros")
        nc.gpsimd.memset(zeros[:].bitcast(I32), 0)
        ident = const.tile([P, P], F32, name="ident")
        make_identity(nc, ident[:])
        nc.gpsimd.memset(staged_scales[:].bitcast(I32), 0)
        ident_bf16 = const.tile([P, P], BF16, name="ident_bf16")
        make_identity(nc, ident_bf16[:])

        load_first_rows()
        x_rows = const.tile([P, D], BF16, name="x_rows")
        xv_rows = const.tile([P, D], BF16, name="xv_rows")

        def place_scales(planes, first):
            for r in range(4):
                begin = first + 2 * r
                nc.sync.dma_start(
                    out=planes[r:P:4, :].bitcast(I32), in_=staged_scales[begin : begin + 32, :].bitcast(I32)
                )

        load_rows(1)
        nc.sync.dma_start(out=x_rows[:], in_=x)
        load_rows(2)
        nc.sync.dma_start(out=xv_rows[:], in_=x_var)
        for g in range(PASSES):
            begin = 32 * (g // 2) + g % 2
            nc.sync.dma_start(
                out=staged_scales[begin : begin + 32 : 2, :]
                .bitcast(I32)
                .rearrange("b (c w) -> b c w", c=CLASSES),
                in_=scale_view[16 * g : 16 * g + 16].bitcast(I32),
            )
        load_rows(3)
        load_rows(4)
        load_rows(5)
        place_scales(run_planes, 0)
        place_scales(plain_planes, 32)

        swapped = const.tile([P, 2, 2, P], F32, name="swapped")
        xv_grouped = const.tile([P, PASSES, P, PACK], BF16, name="xv_grouped", align_bytes=64)
        x_grouped = const.tile([P, 6, P, PACK], BF16, name="x_grouped", align_bytes=64)
        xv_codes = const.tile([P, PASSES, P], U32, name="xv_codes", align_bytes=64)
        x_codes = const.tile([P, 6, P], U32, name="x_codes", align_bytes=64)
        xv_planes = const.tile([P, PASSES, P], U8, name="xv_planes", align_bytes=64)
        x_planes = const.tile([P, 6, P], U8, name="x_planes", align_bytes=64)
        xv_sum = const.tile([P, 1], F32, name="xv_sum")
        pixel_term = const.tile([P, 1], F32, name="pixel_term")

        def sort_x():
            source = x_rows[:, : D // 2].bitcast(F32).rearrange("p (g s h u) -> p h g u s", g=2, h=2, u=2)
            dest = swapped[:].rearrange("p g u (s h) -> p h g u s", h=2)
            for h in range(2):
                nc.vector.tensor_copy(out=dest[:, h], in_=source[:, 1 - h])

        x_banks = {}

        def transpose_x(b):
            bank = banks.tile([P, GROUP], F32, name="bank")
            x_words = x_rows[:].bitcast(F32)
            pass_of = {0: 0, 2: 1, 4: 2, 5: 3}
            transpose_four(
                bank,
                [
                    swapped[:, tile_index // 2, u, :]
                    if tile_index in (1, 3)
                    else x_words[:, 2 * P * pass_of[tile_index] + u : 2 * P * (pass_of[tile_index] + 1) : 2]
                    for u in range(2)
                    for tile_index in (2 * b, 2 * b + 1)
                ],
            )
            x_banks[b] = bank

        def copy_x(b):
            nc.vector.tensor_copy(
                out=x_grouped[:, 2 * b : 2 * b + 2, :, :]
                .bitcast(F32)
                .rearrange("p g n u -> p (g n) u"),
                in_=x_banks[b][:].rearrange("p (u c) -> p c u", u=2),
            )

        def quantise_x():
            for tiles in (slice(0, 4), slice(4, 6)):
                quantise(
                    x_grouped[:, tiles].rearrange("p g n t -> p (g n t)"),
                    x_codes[:, tiles].rearrange("p g n -> p (g n)"),
                    x_planes[:, tiles].rearrange("p g n -> p (g n)"),
                )

        def zero_other_halves():
            for ab in range(2):
                nc.sync.dma_start(
                    out=x_codes[1 - ab : P : 2, 2 * ab : 2 * ab + 2, :].bitcast(I32),
                    in_=zeros[1 - ab : P : 2, :, :].bitcast(I32),
                )

        def transpose_xv_and_root():
            xv_words = xv_rows[:].bitcast(F32)
            for half in range(2):
                bank = banks.tile([P, GROUP], F32, name="bank")
                transpose_four(
                    bank,
                    [
                        xv_words[:, (2 * g + u) * P : (2 * g + u + 1) * P]
                        for u in range(2)
                        for g in (2 * half, 2 * half + 1)
                    ],
                )
                nc.scalar.activation(
                    out=xv_grouped[:, 2 * half : 2 * half + 2, :, :].rearrange(
                        "p g n (u e) -> p (g n) u e", u=2
                    ),
                    in_=bank[:].bitcast(BF16).rearrange("p (u c e) -> p c u e", u=2, e=2),
                    func=SQRT,
                    scale=LAM * LAM,
                )

        def quantise_xv():
            quantise(
                xv_grouped[:].rearrange("p g n t -> p (g n t)"),
                xv_codes[:].rearrange("p g n -> p (g n)"),
                xv_planes[:].rearrange("p g n -> p (g n)"),
            )

        def make_pixel_term():
            sum_row(
                xv_rows[:, : D // 2].rearrange("p (h k) -> p h k", h=2),
                xv_rows[:, D // 2 :].rearrange("p (h k) -> p h k", h=2),
                xv_sum[:],
            )
            nc.vector.tensor_scalar(
                out=pixel_term[:],
                in0=xv_sum[:],
                scalar1=LAM,
                scalar2=2.0,
                op0=ALU.mult,
                op1=ALU.add,
            )

        grouped_of = {}
        sums_of = {}
        codes_of = {}
        planes_of = {}
        spread_of = {}
        shift_of = {}
        acc_of = {}

        def transpose_and_root(unit, g):
            if g == 0:
                grouped_of[unit] = grouped_pool.tile(
                    [P, PASSES, UNIT, PACK], BF16, name="grouped", align_bytes=64
                )
            bank = banks.tile([P, GROUP], F32, name="bank")
            transpose_four(
                bank,
                [
                    rows_of[unit][:, g, t, :].bitcast(F32)[:, u * P : (u + 1) * P]
                    for t in range(2)
                    for u in range(2)
                ],
            )
            nc.scalar.activation(
                out=grouped_of[unit][:, g, :, :]
                .rearrange("p c q -> p (c q)")
                .rearrange("p (r s e) -> p r s e", s=4, e=2),
                in_=bank[:].bitcast(BF16).rearrange("p (s r e) -> p r s e", s=4, e=2),
                func=SQRT,
            )

        def sum_tile(tile_index):
            unit, t = tile_index // 2, tile_index % 2
            group, column = tile_index // 4, tile_index % 4
            if column == 0:
                sums_of[group] = work.tile([P, 4], F32, name="sums", bufs=3)
            sum_row(
                rows_of[unit][:, 0:2, t, :],
                rows_of[unit][:, 2:4, t, :],
                sums_of[group][:, column : column + 1],
            )

        def new_codes(unit):
            codes_of[unit] = codes_pool.tile([P, PASSES, UNIT], U32, name="codes", align_bytes=64)
            planes_of[unit] = codes_pool.tile([P, PASSES, UNIT], U8, name="planes", align_bytes=64)

        def quantise_unit(unit):
            new_codes(unit)
            quantise(
                grouped_of[unit][:].rearrange("p g c t -> p (g c t)"),
                codes_of[unit][:].rearrange("p g c -> p (g c)"),
                planes_of[unit][:].rearrange("p g c -> p (g c)"),
            )

        def quantise_part(unit, g):
            if g == 0:
                new_codes(unit)
            quantise(
                grouped_of[unit][:, g, :, :].rearrange("p c t -> p (c t)"),
                codes_of[unit][:, g, :],
                planes_of[unit][:, g, :],
            )

        def sort_words(group):
            nc.vector.tensor_copy(
                out=words_of[group][:, 0:2].bitcast(I32),
                in_=raw_of[group][:].bitcast(I32).rearrange("p c (j m) -> p j c m", j=2),
            )

        def new_spread(group):
            spread_of[group] = spread_pool.tile([P, GROUP], F32, name="spread")

        def fold_tile(group):
            unit = 2 * group + 1
            new_spread(group)
            for c in range(D // P):
                g, k = c // 4, c % 4 * P
                nc.tensor.matmul(
                    spread_of[group][:, 3 * P :],
                    lhsT=ident_bf16[:],
                    rhs=rows_of[unit][:, g, 1, k : k + P],
                    start=(c == 0),
                    stop=(c == D // P - 1),
                )

        def sum_folded(group):
            nc.vector.tensor_reduce(
                out=sums_of[group][:, 3:4], in_=spread_of[group][:, 3 * P :], op=ALU.add, axis=AXIS_X
            )

        def spread_sums(group):
            if group not in FOLDED:
                new_spread(group)
            for column in range(4):
                nc.tensor.transpose(
                    spread_of[group][:, column * P : (column + 1) * P],
                    sums_of[group][:, column : column + 1].to_broadcast([P, P]),
                    ident[:],
                )

        def make_shift(group):
            shift = work.tile([P, GROUP], F32, name="shift", bufs=4)
            nc.vector.tensor_scalar(
                out=shift[:].rearrange("p (a r t) -> p a r t", a=2, t=2),
                in0=spread_of[group][:].rearrange("p (a t r) -> p a r t", a=2, t=2),
                scalar1=LAM,
                scalar2=pixel_term[:, 0:1],
                op0=ALU.mult,
                op1=ALU.add,
            )
            shift_of[group] = shift

        def accumulator(unit):
            group, half = unit // 2, unit % 2
            if group == N_GROUPS - 1:
                if unit not in acc_of:
                    acc_of[unit] = acc_pool.tile([P, GROUP], F32, name="acc")
                return acc_of[unit][:, :UNIT]
            if group not in acc_of:
                acc_of[group] = acc_pool.tile([P, GROUP], F32, name="acc")
            return acc_of[group][:, half * UNIT : (half + 1) * UNIT]

        def order_of(unit):
            return (4, 5, 6, 7, 0, 1, 2, 8, 9, 3) if unit == N_UNITS - 1 else tuple(range(UNIT_PASSES))

        def multiply(unit, number):
            group, first = unit // 2, unit % 2 * UNIT
            column = group * GROUP + first
            if number < 4:
                left, left_plane = xv_codes[:, number, :], xv_planes[:, number, :]
                right, right_plane = codes_of[unit][:, number, :], planes_of[unit][:, number, :]
            else:
                if number < 8:
                    j, ab = number // 2 % 2, number % 2
                    tile_index, which, plane, scales = 2 * ab + (ab + j) % 2, j, ab, run_planes
                else:
                    tile_index, which, plane, scales = number - 4, number - 6, number - 8, plain_planes
                left, left_plane = x_codes[:, tile_index, :], x_planes[:, tile_index, :]
                right = words_of[group][:, which].rearrange("p c m -> p (c m)")[:, first : first + UNIT]
                right_plane = scales[4 * plane : P, column : column + UNIT]
            nc.tensor.matmul_mx(
                out=accumulator(unit),
                lhsT=left.bitcast(FP8X4),
                lhsT_scale=left_plane,
                rhs=right.bitcast(FP8X4),
                rhs_scale=right_plane,
                start=(number == order_of(unit)[0]),
                stop=(number == order_of(unit)[-1]),
            )

        def finish(acc, shift, first, width):
            result = work.tile([P, GROUP], F32, name="result", bufs=4)
            nc.vector.scalar_tensor_tensor(
                out=result[:, :width],
                in0=acc,
                scalar=2.0,
                in1=shift,
                op0=ALU.mult,
                op1=ALU.subtract,
            )
            nc.sync.dma_start(out=out_cols[:, first : first + width], in_=result[:, :width])

        def finish_group(group):
            finish(acc_of[group][:], shift_of[group][:], group * GROUP, GROUP)

        def finish_unit(unit):
            half = unit % 2
            shift = shift_of[unit // 2][:, half * UNIT : (half + 1) * UNIT]
            finish(acc_of[unit][:, :UNIT], shift, unit * UNIT, UNIT)

        last = N_UNITS - 1
        products = [(unit, number) for unit in range(last - 1) for number in order_of(unit)]
        products += [(last - 1, number) for number in range(4)]
        products = products[: -LEFT]
        half_slots = 2 * N_UNITS - FIRST
        products_at = {}
        for half_slot in range(FIRST, 2 * N_UNITS):
            begin = len(products) * (half_slot - FIRST) // half_slots
            end = len(products) * (half_slot + 1 - FIRST) // half_slots
            products_at[half_slot] = products[begin:end]

        def half_slot_of(product):
            return ([h for h in products_at if product in products_at[h]] + [2 * N_UNITS])[0]

        sorts_at = {half_slot_of((2 * group, 4)) - 1: group for group in range(N_GROUPS - 1)}
        finishes_at = {half_slot_of((2 * group + 1, 9)) // 2 + 1: group for group in range(N_GROUPS - 1)}
        loads_at = {
            2: [(load_words, 0), (load_rows, 6), (load_words, 1), (load_rows, 7), (load_words, 2), (load_rows, 8)],
            3: [(load_rows, 9)],
        }
        for group in range(3, N_GROUPS):
            slot = half_slot_of((2 * group - 5, 9)) // 2
            loads_at.setdefault(slot, []).append((load_words, group))
            for unit in range(2 * group + 4, min(2 * group + 6, N_UNITS)):
                loads_at[slot].append((load_rows, unit))

        on_vector = [t for t in range(2 * N_UNITS) if not (t % 4 == 3 and t // 4 in FOLDED)]
        even_from = 2 * FOLDED[0]
        later = on_vector[2 * even_from :]

        def tiles_of(slot):
            if slot < even_from:
                return on_vector[2 * slot : 2 * slot + 2]
            ends = [len(later) * (s - even_from) // (last - even_from) for s in (slot, slot + 1)]
            return later[ends[0] : ends[1]]

        for slot in range(N_UNITS):
            tiles = tiles_of(slot)
            for tile_index in tiles[:1]:
                sum_tile(tile_index)
            if slot >= 1:
                quantise_unit(slot - 1)
            if slot == 1:
                sort_x()
            if slot == 2:
                make_pixel_term()
                quantise_xv()
            for half in range(2):
                for g in (2 * half, 2 * half + 1):
                    transpose_and_root(slot, g)
                if 3 <= 2 * slot + half < 6:
                    transpose_x(2 * slot + half - 3)
                    copy_x(2 * slot + half - 3)
                if half == 1 and slot >= 2 and slot % 2 == 0:
                    spread_sums(slot // 2 - 1)
                if half == 1 and slot == last:
                    sum_folded(N_GROUPS - 1)
                    spread_sums(N_GROUPS - 1)
                if 2 * slot + half in sorts_at:
                    sort_words(sorts_at[2 * slot + half])
                for unit, number in products_at.get(2 * slot + half, []):
                    multiply(unit, number)
                if half == 0 and slot % 2 == 1 and slot // 2 in FOLDED:
                    fold_tile(slot // 2)
            if slot == 1:
                transpose_xv_and_root()
            for tile_index in tiles[1:]:
                sum_tile(tile_index)
            if slot % 2 == 1 and slot // 2 in FOLDED and slot < last:
                sum_folded(slot // 2)
            if slot == 2:
                quantise_x()
                zero_other_halves()
            if slot >= 2 and slot % 2 == 0:
                make_shift(slot // 2 - 1)
            if slot in finishes_at:
                finish_group(finishes_at[slot])
            if slot == last:
                sort_words(N_GROUPS - 1)
                make_shift(N_GROUPS - 1)
                quantise_part(last, 0)
                quantise_part(last, 1)
            for load, number in loads_at.get(slot, []):
                load(number)

        done = set(products)
        for unit in (last - 2, last - 1):
            for number in order_of(unit)[: 8 if unit == last - 1 else 10]:
                if (unit, number) not in done:
                    multiply(unit, number)
        for number in order_of(last)[:4]:
            multiply(last, number)
        quantise_part(last, 2)
        finish_group(N_GROUPS - 2)
        quantise_part(last, 3)
        for number in order_of(last)[4:7]:
            multiply(last, number)
        for number in (8, 9):
            multiply(last - 1, number)
        finish_unit(last - 1)
        for number in order_of(last)[7:]:
            multiply(last, number)
        finish_unit(last)
